import numpy as np
import ml_dtypes


def mxq(x, axis, fmt="e4m3"):
    dtype, down = {"e4m3": (ml_dtypes.float8_e4m3fn, 7), "e5m2": (ml_dtypes.float8_e5m2, 14)}[fmt]
    v = np.moveaxis(np.asarray(x, np.float32).astype(ml_dtypes.bfloat16).astype(np.float64), axis, -1)
    blocks = v.reshape(v.shape[:-1] + (-1, 32))
    amax = np.abs(blocks).max(-1, keepdims=True)
    byte = np.maximum(np.where(amax > 0, np.frexp(amax)[1] - 1 + 127, 0) - down, 1)
    scale = np.exp2(byte - 127.0)
    codes = (blocks / scale).astype(np.float32).astype(dtype).astype(np.float64)
    return np.moveaxis((codes * scale).reshape(v.shape), -1, axis)


WIDE = False


def mx_kscale(k):
    if not WIDE:
        return np.ones(k)
    levels = np.array([10, -10, 5, -5, 0])
    a = np.random.permutation(np.resize(levels, k // 512 * 4)).reshape(k // 512, 4)
    idx = np.arange(k)
    return np.exp2(a[idx // 512, idx % 128 // 32])


BF16 = ml_dtypes.bfloat16


def bf(x):
    return np.asarray(x, np.float32).astype(BF16)


def f64(x):
    return np.asarray(x).astype(np.float64)


B, C, H, W = 128, 512, 6, 6
C3, P = 3 * C, H * W
EPS = 1e-5


def setup_inputs():
    s = mx_kscale(C3)
    n = np.random.standard_normal
    return {
        "fv": bf(n((B, C3, H, W)) * s[None, :, None, None]),
        "ft": bf(n((B, C))),
        "W1": bf(n((C, C3)) / np.sqrt(C3) / s[None, :]),
        "b1": bf(n(C) * 0.3),
        "g1": bf(1.0 + 0.1 * n(C)),
        "be1": bf(n(C) * 0.3),
        "m1": bf(n(C) * 0.3),
        "v1": bf(np.random.uniform(0.5, 1.5, C)),
        "Wfc1": bf(n((C, C)) * 0.7 / np.sqrt(C)),
        "bfc1": bf(n(C) * 0.3),
    }


def reference(fv, ft, W1, b1, g1, be1, m1, v1, Wfc1, bfc1):
    x = (mxq(f64(W1), 1, "e4m3") @ mxq(f64(fv).reshape(B, C3, P), 1, "e4m3")) + f64(b1)[None, :, None]
    s = f64(g1) / np.sqrt(f64(v1) + EPS)
    fv1 = np.maximum(x * s[None, :, None] + (f64(be1) - f64(m1) * s)[None, :, None], 0.0)
    ft1 = f64(ft) @ f64(Wfc1).T + f64(bfc1)
    out = fv1 + fv1 * ft1[:, :, None]
    return out.reshape(B, C, H, W)

@@ -1,0 +1,239 @@
+from contextlib import ExitStack
+
+import concourse.bass as bass
+import concourse.mybir as mybir
+import concourse.tile as tile
+from concourse.masks import make_identity
+
+F32 = mybir.dt.float32
+BF16 = mybir.dt.bfloat16
+U32 = mybir.dt.uint32
+U8 = mybir.dt.uint8
+FP8X4 = mybir.dt.float8_e4m3fn_x4
+ALU = mybir.AluOpType
+ACT = mybir.ActivationFunctionType
+
+P = 128
+B, C, PX = 128, 512, 36
+C3 = 3 * C
+EPS = 1e-5
+NG = 3
+NJ = 4
+CB = 32
+NCH = B // CB
+XA = 32
+XB = PX - XA
+HB = 16
+COLS = CB * PX
+CA = CB * XA
+
+FLOPS = 2 * C * C3 * B * PX + 2 * B * C * C
+
+
+def tile_joint_module_pa_t_kernel(tc, fv, ft, W1, b1, g1, be1, m1, v1, Wfc1, bfc1, out):
+    nc = tc.nc
+    with ExitStack() as keep_ctx:
+        keep = keep_ctx.enter_context(tc.tile_pool(name="keep", bufs=1))
+        ps_acc = keep_ctx.enter_context(tc.psum_pool(name="ps_acc", bufs=4))
+        ps_nar = keep_ctx.enter_context(tc.psum_pool(name="ps_nar", bufs=2))
+        ps_set = keep_ctx.enter_context(tc.psum_pool(name="ps_set", bufs=2))
+
+        ident_bf = keep.tile([P, P], BF16)
+        make_identity(nc, ident_bf[:])
+        ident_f = keep.tile([P, P], F32)
+        make_identity(nc, ident_f[:])
+        ones_bf = keep.tile([P, P], BF16)
+        nc.vector.memset(ones_bf[:], 1.0)
+
+        y = keep.tile([P, NJ, PX, B], F32)
+        w_codes = keep.tile([P, NG, C], U32, align_bytes=64)
+        w_scales = keep.tile([P, NG, C], U8, align_bytes=64)
+        gate = keep.tile([P, C], F32)
+        bn_scale = keep.tile([P, NJ], F32)
+        bn_shift = keep.tile([P, NJ], F32)
+
+        with ExitStack() as run_ctx:
+            setup = run_ctx.enter_context(tc.tile_pool(name="setup", bufs=1))
+            wg_pool = run_ctx.enter_context(tc.tile_pool(name="wg", bufs=2))
+            raw_pool = run_ctx.enter_context(tc.tile_pool(name="raw", bufs=5))
+            grp_pool = run_ctx.enter_context(tc.tile_pool(name="grp", bufs=3))
+            code_pool = run_ctx.enter_context(tc.tile_pool(name="code", bufs=2))
+
+            w1_sb = setup.tile([P, NJ * C3], BF16)
+            nc.sync.dma_start(
+                out=w1_sb[:].rearrange("o (j c) -> o j c", j=NJ),
+                in_=W1.rearrange("(j o) c -> o j c", j=NJ),
+            )
+            vec_rows = setup.tile([P, P], BF16)
+            nc.vector.memset(vec_rows[:], 0.0)
+            for i, vec in enumerate((b1, g1, be1, m1, v1)):
+                nc.scalar.dma_start(
+                    out=vec_rows[NJ * i : NJ * (i + 1), :],
+                    in_=vec.rearrange("(j c) -> j c", j=NJ),
+                )
+            bias_row = setup.tile([P, C], BF16)
+            nc.vector.memset(bias_row[:], 0.0)
+            nc.scalar.dma_start(out=bias_row[0:1, :], in_=bfc1.rearrange("(o c) -> o c", o=1))
+            ft_sb = setup.tile([P, C], BF16)
+            nc.scalar.dma_start(out=ft_sb[:], in_=ft)
+            wfc_sb = setup.tile([P, NJ, C], BF16)
+            nc.scalar.dma_start(out=wfc_sb[:], in_=Wfc1.rearrange("(j o) k -> o j k", j=NJ))
+
+            pv = ps_set.tile([P, P], BF16, tag="set")
+            nc.tensor.transpose(pv[:], vec_rows[:], ident_bf[:])
+            vecs = setup.tile([P, 5 * NJ], F32)
+            nc.vector.tensor_copy(out=vecs[:], in_=pv[:, 0 : 5 * NJ])
+            col = lambda i: vecs[:, NJ * i : NJ * (i + 1)]
+            std = setup.tile([P, NJ], F32)
+            nc.vector.tensor_scalar_add(out=std[:], in0=col(4), scalar1=EPS)
+            nc.scalar.sqrt(std[:], std[:])
+            rstd = setup.tile([P, NJ], F32)
+            nc.vector.reciprocal(rstd[:], std[:])
+            nc.vector.tensor_mul(out=bn_scale[:], in0=col(1), in1=rstd[:])
+            diff = setup.tile([P, NJ], F32)
+            nc.vector.tensor_sub(out=diff[:], in0=col(0), in1=col(3))
+            nc.vector.tensor_mul(out=diff[:], in0=diff[:], in1=bn_scale[:])
+            nc.vector.tensor_add(out=bn_shift[:], in0=diff[:], in1=col(2))
+
+            w_words = w1_sb[:].bitcast(F32).rearrange(
+                "o (j g p u) -> o j g u p", j=NJ, g=NG, p=P, u=2
+            )
+            for g in range(NG):
+                wg = wg_pool.tile([P, 4 * C], BF16, align_bytes=64)
+                wg_words = wg[:].bitcast(F32).rearrange("p (j o u) -> p j o u", j=NJ, o=P, u=2)
+                for jp in range(NJ // 2):
+                    pw = ps_set.tile([P, 2, 2, P], F32, tag="set")
+                    for jj in range(2):
+                        for u in range(2):
+                            nc.tensor.transpose(
+                                pw[:, jj, u, :], w_words[:, 2 * jp + jj, g, u, :], ident_f[:]
+                            )
+                    nc.vector.tensor_copy(
+                        out=wg_words[:, 2 * jp : 2 * jp + 2],
+                        in_=pw[:].rearrange("p j u o -> p j o u"),
+                    )
+                nc.vector.quantize_mx(
+                    out=w_codes[:, g, :].bitcast(FP8X4), scales=w_scales[:, g, :], in_=wg[:]
+                )
+
+            ftT = setup.tile([P, NJ, P], BF16)
+            pt = ps_set.tile([P, NJ, P], BF16, tag="set")
+            for kc in range(NJ):
+                nc.tensor.transpose(pt[:, kc, :], ft_sb[:, kc * P : (kc + 1) * P], ident_bf[:])
+            nc.vector.tensor_copy(out=ftT[:], in_=pt[:])
+            wfcT = setup.tile([P, NJ, C], BF16)
+            for kc in range(NJ):
+                pk = ps_set.tile([P, NJ, P], BF16, tag="set")
+                for j in range(NJ):
+                    nc.tensor.transpose(pk[:, j, :], wfc_sb[:, j, kc * P : (kc + 1) * P], ident_bf[:])
+                nc.scalar.copy(out=wfcT[:, kc, :], in_=pk[:].rearrange("p j o -> p (j o)"))
+            pf = ps_set.tile([P, C], F32, tag="set")
+            for kc in range(NJ):
+                nc.tensor.matmul(pf[:], lhsT=ftT[:, kc, :], rhs=wfcT[:, kc, :], start=(kc == 0), stop=False)
+            nc.tensor.matmul(pf[:], lhsT=ones_bf[:], rhs=bias_row[:], start=False, stop=True)
+            nc.vector.tensor_scalar_add(out=gate[:], in0=pf[:], scalar1=1.0)
+
+            state = {}
+
+            def load_and_group(n):
+                ch, g = divmod(n, NG)
+                b0 = ch * CB
+                if g == 0:
+                    codes = code_pool.tile([P, NG, COLS], U32, align_bytes=64)
+                    scales = code_pool.tile([P, NG, COLS], U8, align_bytes=64)
+                    state[ch] = (codes, scales)
+                raw = raw_pool.tile([P, CB, 4, PX], BF16)
+                nc.sync.dma_start(
+                    out=raw[:].rearrange("p b t x -> p b (t x)"),
+                    in_=fv[b0 : b0 + CB, g * C : (g + 1) * C].rearrange(
+                        "b (p t) h w -> p b (t h w)", t=4
+                    ),
+                )
+                grp = grp_pool.tile([P, 4 * COLS], BF16, align_bytes=64)
+                nc.vector.tensor_copy(
+                    out=grp[:, 0 : 4 * CA].rearrange("p (b c i t) -> p b c t i", b=CB, c=XA // 4, i=4, t=4),
+                    in_=raw[:, :, :, 0:XA].rearrange("p b t (c i) -> p b c t i", i=4),
+                )
+                nc.vector.tensor_copy(
+                    out=grp[:, 4 * CA : 4 * COLS].rearrange("p (b i t) -> p b t i", b=CB, i=XB, t=4),
+                    in_=raw[:, :, :, XA:PX],
+                )
+                return grp
+
+            def quantise(n, grp):
+                ch, g = divmod(n, NG)
+                codes, scales = state[ch]
+                nc.vector.quantize_mx(
+                    out=codes[:, g, 0:CA].bitcast(FP8X4), scales=scales[:, g, 0:CA], in_=grp[:, 0 : 4 * CA]
+                )
+                nc.vector.quantize_mx(
+                    out=codes[:, g, CA:COLS].bitcast(FP8X4),
+                    scales=scales[:, g, CA:COLS],
+                    in_=grp[:, 4 * CA : 4 * COLS],
+                )
+
+            def group(acc, j, codes, scales, lo, hi):
+                for g in range(NG):
+                    nc.tensor.matmul_mx(
+                        out=acc,
+                        lhsT=w_codes[:, g, j * P : (j + 1) * P].bitcast(FP8X4),
+                        lhsT_scale=w_scales[:, g, j * P : (j + 1) * P],
+                        rhs=codes[:, g, lo:hi].bitcast(FP8X4),
+                        rhs_scale=scales[:, g, lo:hi],
+                        start=(g == 0),
+                        stop=(g == NG - 1),
+                    )
+
+            def multiply(ch):
+                codes, scales = state[ch]
+                b0 = ch * CB
+                for j in range(NJ):
+                    for s in range(CB // HB):
+                        acc = ps_acc.tile([P, HB * XA], F32, tag="acc")
+                        group(acc[:], j, codes, scales, s * HB * XA, (s + 1) * HB * XA)
+                        nc.scalar.activation(
+                            out=y[:, j, 0:XA, b0 + s * HB : b0 + (s + 1) * HB],
+                            in_=acc[:].rearrange("o (b x) -> o x b", x=XA),
+                            func=ACT.Identity,
+                            bias=bn_shift[:, j : j + 1],
+                            scale=bn_scale[:, j : j + 1],
+                        )
+                    nar = ps_nar.tile([P, CB * XB], F32, tag="nar")
+                    group(nar[:], j, codes, scales, CA, COLS)
+                    nc.scalar.activation(
+                        out=y[:, j, XA:PX, b0 : b0 + CB],
+                        in_=nar[:].rearrange("o (b x) -> o x b", x=XB),
+                        func=ACT.Identity,
+                        bias=bn_shift[:, j : j + 1],
+                        scale=bn_scale[:, j : j + 1],
+                    )
+
+            pieces = NCH * NG
+            last = None
+            for n in range(pieces + 1):
+                grp = load_and_group(n) if n < pieces else None
+                if n >= 1:
+                    quantise(n - 1, last)
+                    if (n - 1) % NG == NG - 1:
+                        multiply((n - 1) // NG)
+                last = grp
+
+        with tc.tile_pool(name="ost", bufs=3) as ost_pool:
+            for j in range(NJ):
+                ost = ost_pool.tile([P, P, PX], F32)
+                for q in range(PX // 4):
+                    tr = ps_acc.tile([P, 4, P], F32, tag="acc")
+                    for x in range(4):
+                        nc.tensor.transpose(tr[:, x, :], y[:, j, 4 * q + x, :], ident_f[:])
+                    nc.vector.scalar_tensor_tensor(
+                        out=ost[:, :, 4 * q : 4 * q + 4],
+                        in0=tr[:].rearrange("b x o -> b o x"),
+                        scalar=0.0,
+                        in1=gate[:, j * P : (j + 1) * P].unsqueeze(2).to_broadcast([P, P, 4]),
+                        op0=ALU.max,
+                        op1=ALU.mult,
+                    )
+                nc.sync.dma_start(
+                    out=out[:, j * P : (j + 1) * P].rearrange("b o h w -> b (o h w)"),
+                    in_=ost[:].rearrange("b o x -> b (o x)"),
+                )

@@ -27,6 +27,10 @@ HB = 16
 COLS = CB * PX
 CA = CB * XA
 
+NQ = PX // 4
+J_ORDER = (0, 3, 1, 2)
+J_VECTOR = (0, 1, 2)
+
 FLOPS = 2 * C * C3 * B * PX + 2 * B * C * C
 
 
@@ -135,71 +139,88 @@ def tile_joint_module_pa_t_kernel(tc, fv, ft, W1, b1, g1, be1, m1, v1, Wfc1, bfc
 
             state = {}
 
-            def load_and_group(n):
-                ch, g = divmod(n, NG)
-                b0 = ch * CB
-                if g == 0:
+            def load_and_group(ch, h, nb, g):
+                b0 = ch * CB + h * HB
+                if h == 0 and g == 0:
                     codes = code_pool.tile([P, NG, COLS], U32, align_bytes=64)
                     scales = code_pool.tile([P, NG, COLS], U8, align_bytes=64)
                     state[ch] = (codes, scales)
-                raw = raw_pool.tile([P, CB, 4, PX], BF16)
+                raw = raw_pool.tile([P, nb, 4, PX], BF16, tag="raw")
                 nc.sync.dma_start(
                     out=raw[:].rearrange("p b t x -> p b (t x)"),
-                    in_=fv[b0 : b0 + CB, g * C : (g + 1) * C].rearrange(
+                    in_=fv[b0 : b0 + nb, g * C : (g + 1) * C].rearrange(
                         "b (p t) h w -> p b (t h w)", t=4
                     ),
                 )
-                grp = grp_pool.tile([P, 4 * COLS], BF16, align_bytes=64)
+                grp = grp_pool.tile([P, 4 * nb * PX], BF16, tag="grp", align_bytes=64)
+                na = 4 * nb * XA
                 nc.vector.tensor_copy(
-                    out=grp[:, 0 : 4 * CA].rearrange("p (b c i t) -> p b c t i", b=CB, c=XA // 4, i=4, t=4),
+                    out=grp[:, 0:na].rearrange("p (b c i t) -> p b c t i", b=nb, c=XA // 4, i=4, t=4),
                     in_=raw[:, :, :, 0:XA].rearrange("p b t (c i) -> p b c t i", i=4),
                 )
-                nc.vector.tensor_copy(
-                    out=grp[:, 4 * CA : 4 * COLS].rearrange("p (b i t) -> p b t i", b=CB, i=XB, t=4),
+                nc.scalar.copy(
+                    out=grp[:, na : 4 * nb * PX].rearrange("p (b i t) -> p b t i", b=nb, i=XB, t=4),
                     in_=raw[:, :, :, XA:PX],
                 )
                 return grp
 
-            def quantise(n, grp):
-                ch, g = divmod(n, NG)
+            def quantise(ch, h, nb, g, grp):
                 codes, scales = state[ch]
+                na = 4 * nb * XA
+                lo, hi = h * HB * XA, (h * HB + nb) * XA
                 nc.vector.quantize_mx(
-                    out=codes[:, g, 0:CA].bitcast(FP8X4), scales=scales[:, g, 0:CA], in_=grp[:, 0 : 4 * CA]
+                    out=codes[:, g, lo:hi].bitcast(FP8X4), scales=scales[:, g, lo:hi], in_=grp[:, 0:na]
                 )
+                lo, hi = CA + h * HB * XB, CA + (h * HB + nb) * XB
                 nc.vector.quantize_mx(
-                    out=codes[:, g, CA:COLS].bitcast(FP8X4),
-                    scales=scales[:, g, CA:COLS],
-                    in_=grp[:, 4 * CA : 4 * COLS],
+                    out=codes[:, g, lo:hi].bitcast(FP8X4),
+                    scales=scales[:, g, lo:hi],
+                    in_=grp[:, na : 4 * nb * PX],
                 )
 
-            def group(acc, j, codes, scales, lo, hi):
+            def mx_pass(acc, j, g, ch, lo, hi):
+                codes, scales = state[ch]
+                nc.tensor.matmul_mx(
+                    out=acc,
+                    lhsT=w_codes[:, g, j * P : (j + 1) * P].bitcast(FP8X4),
+                    lhsT_scale=w_scales[:, g, j * P : (j + 1) * P],
+                    rhs=codes[:, g, lo:hi].bitcast(FP8X4),
+                    rhs_scale=scales[:, g, lo:hi],
+                    start=(g == 0),
+                    stop=(g == NG - 1),
+                )
+
+            def wide_out(acc, j, ch, s):
+                b0 = ch * CB + s * HB
+                nc.scalar.activation(
+                    out=y[:, j, 0:XA, b0 : b0 + HB],
+                    in_=acc[:].rearrange("o (b x) -> o x b", x=XA),
+                    func=ACT.Identity,
+                    bias=bn_shift[:, j : j + 1],
+                    scale=bn_scale[:, j : j + 1],
+                )
+
+            def wide(j, ch, s):
+                acc = ps_acc.tile([P, HB * XA], F32, tag="acc")
                 for g in range(NG):
-                    nc.tensor.matmul_mx(
-                        out=acc,
-                        lhsT=w_codes[:, g, j * P : (j + 1) * P].bitcast(FP8X4),
-                        lhsT_scale=w_scales[:, g, j * P : (j + 1) * P],
-                        rhs=codes[:, g, lo:hi].bitcast(FP8X4),
-                        rhs_scale=scales[:, g, lo:hi],
-                        start=(g == 0),
-                        stop=(g == NG - 1),
-                    )
+                    mx_pass(acc[:], j, g, ch, s * HB * XA, (s + 1) * HB * XA)
+                wide_out(acc, j, ch, s)
 
-            def multiply(ch):
-                codes, scales = state[ch]
+            def narrow(j, ch, on_vector):
                 b0 = ch * CB
-                for j in range(NJ):
-                    for s in range(CB // HB):
-                        acc = ps_acc.tile([P, HB * XA], F32, tag="acc")
-                        group(acc[:], j, codes, scales, s * HB * XA, (s + 1) * HB * XA)
-                        nc.scalar.activation(
-                            out=y[:, j, 0:XA, b0 + s * HB : b0 + (s + 1) * HB],
-                            in_=acc[:].rearrange("o (b x) -> o x b", x=XA),
-                            func=ACT.Identity,
-                            bias=bn_shift[:, j : j + 1],
-                            scale=bn_scale[:, j : j + 1],
-                        )
-                    nar = ps_nar.tile([P, CB * XB], F32, tag="nar")
-                    group(nar[:], j, codes, scales, CA, COLS)
+                nar = ps_nar.tile([P, CB * XB], F32, tag="nar")
+                for g in range(NG):
+                    mx_pass(nar[:], j, g, ch, CA, COLS)
+                if on_vector:
+                    nc.vector.tensor_scalar(
+                        out=y[:, j, XA:PX, b0 : b0 + CB],
+                        in0=nar[:].rearrange("o (b x) -> o x b", x=XB),
+                        scalar1=bn_scale[:, j : j + 1],
+                        scalar2=bn_shift[:, j : j + 1],
+                        op0=ALU.mult,
+                        op1=ALU.add,
+                    )
+                else:
                     nc.scalar.activation(
                         out=y[:, j, XA:PX, b0 : b0 + CB],
                         in_=nar[:].rearrange("o (b x) -> o x b", x=XB),
@@ -208,32 +229,85 @@ def tile_joint_module_pa_t_kernel(tc, fv, ft, W1, b1, g1, be1, m1, v1, Wfc1, bfc
                         scale=bn_scale[:, j : j + 1],
                     )
 
-            pieces = NCH * NG
+            LAST = NCH - 1
+            open_acc = {}
+
+            def after(ch, h, nb, g):
+                if ch < LAST:
+                    if g == NG - 1:
+                        for j in range(NJ):
+                            wide(j, ch, 0)
+                            wide(j, ch, 1)
+                            narrow(j, ch, False)
+                elif h == 0:
+                    if g == NG - 1:
+                        for j in range(NJ):
+                            wide(j, ch, 0)
+                else:
+                    for j in J_ORDER:
+                        if g == 0:
+                            acc = ps_acc.tile([P, HB * XA], F32, tag="acc")
+                            open_acc[j] = acc
+                        mx_pass(open_acc[j][:], j, g, ch, HB * XA, 2 * HB * XA)
+                        if g == NG - 1:
+                            wide_out(open_acc[j], j, ch, 1)
+                            narrow(j, ch, True)
+
+            plan = [(ch, 0, CB, g) for ch in range(LAST) for g in range(NG)]
+            plan += [(LAST, h, HB, g) for h in range(2) for g in range(NG)]
             last = None
-            for n in range(pieces + 1):
-                grp = load_and_group(n) if n < pieces else None
+            for n in range(len(plan) + 1):
+                grp = load_and_group(*plan[n]) if n < len(plan) else None
                 if n >= 1:
-                    quantise(n - 1, last)
-                    if (n - 1) % NG == NG - 1:
-                        multiply((n - 1) // NG)
+                    quantise(*plan[n - 1], last)
+                    after(*plan[n - 1])
                 last = grp
 
-        with tc.tile_pool(name="ost", bufs=3) as ost_pool:
-            for j in range(NJ):
-                ost = ost_pool.tile([P, P, PX], F32)
-                for q in range(PX // 4):
-                    tr = ps_acc.tile([P, 4, P], F32, tag="acc")
-                    for x in range(4):
-                        nc.tensor.transpose(tr[:, x, :], y[:, j, 4 * q + x, :], ident_f[:])
-                    nc.vector.scalar_tensor_tensor(
-                        out=ost[:, :, 4 * q : 4 * q + 4],
-                        in0=tr[:].rearrange("b x o -> b o x"),
-                        scalar=0.0,
-                        in1=gate[:, j * P : (j + 1) * P].unsqueeze(2).to_broadcast([P, P, 4]),
-                        op0=ALU.max,
-                        op1=ALU.mult,
-                    )
+        with tc.tile_pool(name="ost", bufs=4) as ost_pool, tc.tile_pool(name="tmp", bufs=3) as tmp_pool:
+            osts = {}
+
+            def turn(pool, tag, j, q):
+                if q == 0:
+                    ost = ost_pool.tile([P, P, PX], F32, tag="ost")
+                    osts[j] = ost
+                tr = pool.tile([P, 4, P], F32, tag=tag)
+                for x in range(4):
+                    nc.tensor.transpose(tr[:, x, :], y[:, j, 4 * q + x, :], ident_f[:])
+                return tr
+
+            def store(j):
                 nc.sync.dma_start(
                     out=out[:, j * P : (j + 1) * P].rearrange("b o h w -> b (o h w)"),
-                    in_=ost[:].rearrange("b o x -> b (o x)"),
+                    in_=osts[j][:].rearrange("b o x -> b (o x)"),
                 )
+
+            def gate_of(j):
+                return gate[:, j * P : (j + 1) * P].unsqueeze(2).to_broadcast([P, P, 4])
+
+            def on_vector(j, q):
+                tr = turn(ps_acc, "acc", j, q)
+                nc.vector.scalar_tensor_tensor(
+                    out=osts[j][:, :, 4 * q : 4 * q + 4],
+                    in0=tr[:].rearrange("b x o -> b o x"),
+                    scalar=0.0,
+                    in1=gate_of(j),
+                    op0=ALU.max,
+                    op1=ALU.mult,
+                )
+                if q == NQ - 1:
+                    store(j)
+
+            def on_scalar_gpsimd(j, q):
+                tr = turn(ps_set, "set", j, q)
+                tmp = tmp_pool.tile([P, P, 4], F32, tag="tmp")
+                nc.scalar.activation(out=tmp[:], in_=tr[:].rearrange("b x o -> b o x"), func=ACT.Relu)
+                nc.gpsimd.tensor_tensor(
+                    out=osts[j][:, :, 4 * q : 4 * q + 4], in0=tmp[:], in1=gate_of(j), op=ALU.mult
+                )
+                if q == NQ - 1:
+                    store(j)
+
+            for i in range(3 * NQ):
+                if i % 3 == 0:
+                    on_scalar_gpsimd(J_ORDER[1], i // 3)
+                on_vector(J_VECTOR[i // NQ], i % NQ)

@@ -28,6 +28,7 @@ COLS = CB * PX
 CA = CB * XA
 
 NQ = PX // 4
+KEEP_N = 64
 J_ORDER = (0, 3, 1, 2)
 J_VECTOR = (0, 1, 2)
 
@@ -273,6 +274,8 @@ def tile_joint_module_pa_t_kernel(tc, fv, ft, W1, b1, g1, be1, m1, v1, Wfc1, bfc
                 tr = pool.tile([P, 4, P], F32, tag=tag)
                 for x in range(4):
                     nc.tensor.transpose(tr[:, x, :], y[:, j, 4 * q + x, :], ident_f[:])
+                idle = ps_nar.tile([P, KEEP_N], F32, tag="nar")
+                nc.tensor.matmul(idle[:], lhsT=ident_f[:], rhs=y[:, j, 4 * q, 0:KEEP_N], start=True, stop=True)
                 return tr
 
             def store(j):

@@ -1,8 +1,6 @@
 from contextlib import ExitStack
 
-import concourse.bass as bass
 import concourse.mybir as mybir
-import concourse.tile as tile
 from concourse.masks import make_identity
 
 F32 = mybir.dt.float32
@@ -21,16 +19,13 @@ NG = 3
 NJ = 4
 CB = 32
 NCH = B // CB
-XA = 32
-XB = PX - XA
-HB = 16
-COLS = CB * PX
-CA = CB * XA
-
 NQ = PX // 4
-KEEP_N = 64
+COLS = CB * PX
+QCOLS = CB * 4
+WIDE = 4 * QCOLS
 J_ORDER = (0, 3, 1, 2)
 J_VECTOR = (0, 1, 2)
+G_ORDER = (2, 0, 1)
 
 FLOPS = 2 * C * C3 * B * PX + 2 * B * C * C
 
@@ -42,6 +37,9 @@ def tile_joint_module_pa_t_kernel(tc, fv, ft, W1, b1, g1, be1, m1, v1, Wfc1, bfc
         ps_acc = keep_ctx.enter_context(tc.psum_pool(name="ps_acc", bufs=4))
         ps_nar = keep_ctx.enter_context(tc.psum_pool(name="ps_nar", bufs=2))
         ps_set = keep_ctx.enter_context(tc.psum_pool(name="ps_set", bufs=2))
+        big_pool = keep_ctx.enter_context(tc.tile_pool(name="big", bufs=3))
+        grp_pool = keep_ctx.enter_context(tc.tile_pool(name="grp", bufs=3))
+        code_pool = keep_ctx.enter_context(tc.tile_pool(name="code", bufs=2))
 
         ident_bf = keep.tile([P, P], BF16)
         make_identity(nc, ident_bf[:])
@@ -50,19 +48,32 @@ def tile_joint_module_pa_t_kernel(tc, fv, ft, W1, b1, g1, be1, m1, v1, Wfc1, bfc
         ones_bf = keep.tile([P, P], BF16)
         nc.vector.memset(ones_bf[:], 1.0)
 
-        y = keep.tile([P, NJ, PX, B], F32)
         w_codes = keep.tile([P, NG, C], U32, align_bytes=64)
         w_scales = keep.tile([P, NG, C], U8, align_bytes=64)
+        codes2 = keep.tile([P, NCH, COLS], U32, align_bytes=64)
+        scales2 = keep.tile([P, NCH, COLS], U8, align_bytes=64)
         gate = keep.tile([P, C], F32)
         bn_scale = keep.tile([P, NJ], F32)
         bn_shift = keep.tile([P, NJ], F32)
 
-        with ExitStack() as run_ctx:
-            setup = run_ctx.enter_context(tc.tile_pool(name="setup", bufs=1))
-            wg_pool = run_ctx.enter_context(tc.tile_pool(name="wg", bufs=2))
-            raw_pool = run_ctx.enter_context(tc.tile_pool(name="raw", bufs=5))
-            grp_pool = run_ctx.enter_context(tc.tile_pool(name="grp", bufs=3))
-            code_pool = run_ctx.enter_context(tc.tile_pool(name="code", bufs=2))
+        raws = {}
+
+        def load_chunk(ch):
+            b0 = ch * CB
+            raw = big_pool.tile([P, 2, CB, 4, PX], BF16, tag="big")
+            for g in range(2):
+                nc.sync.dma_start(
+                    out=raw[:, g].rearrange("p b t x -> p b (t x)"),
+                    in_=fv[b0 : b0 + CB, g * C : (g + 1) * C].rearrange(
+                        "b (p t) h w -> p b (t h w)", t=4
+                    ),
+                )
+            raws[ch] = raw
+
+        with ExitStack() as a_ctx:
+            setup = a_ctx.enter_context(tc.tile_pool(name="setup", bufs=1))
+            wg_pool = a_ctx.enter_context(tc.tile_pool(name="wg", bufs=2))
+            g2_pool = a_ctx.enter_context(tc.tile_pool(name="g2", bufs=3))
 
             w1_sb = setup.tile([P, NJ * C3], BF16)
             nc.sync.dma_start(
@@ -83,6 +94,14 @@ def tile_joint_module_pa_t_kernel(tc, fv, ft, W1, b1, g1, be1, m1, v1, Wfc1, bfc
             nc.scalar.dma_start(out=ft_sb[:], in_=ft)
             wfc_sb = setup.tile([P, NJ, C], BF16)
             nc.scalar.dma_start(out=wfc_sb[:], in_=Wfc1.rearrange("(j o) k -> o j k", j=NJ))
+            x2 = setup.tile([P, C * PX], BF16)
+            for t in range(4):
+                nc.sync.dma_start(
+                    out=x2[:, t * P * PX : (t + 1) * P * PX],
+                    in_=fv[:, 2 * C + t * P : 2 * C + (t + 1) * P].rearrange("b c h w -> b (c h w)"),
+                )
+            for ch in range(3):
+                load_chunk(ch)
 
             pv = ps_set.tile([P, P], BF16, tag="set")
             nc.tensor.transpose(pv[:], vec_rows[:], ident_bf[:])
@@ -103,8 +122,8 @@ def tile_joint_module_pa_t_kernel(tc, fv, ft, W1, b1, g1, be1, m1, v1, Wfc1, bfc
             w_words = w1_sb[:].bitcast(F32).rearrange(
                 "o (j g p u) -> o j g u p", j=NJ, g=NG, p=P, u=2
             )
-            for g in range(NG):
-                wg = wg_pool.tile([P, 4 * C], BF16, align_bytes=64)
+            for g in range(2):
+                wg = wg_pool.tile([P, 4 * C], BF16, tag="wg", align_bytes=64)
                 wg_words = wg[:].bitcast(F32).rearrange("p (j o u) -> p j o u", j=NJ, o=P, u=2)
                 for jp in range(NJ // 2):
                     pw = ps_set.tile([P, 2, 2, P], F32, tag="set")
@@ -120,6 +139,17 @@ def tile_joint_module_pa_t_kernel(tc, fv, ft, W1, b1, g1, be1, m1, v1, Wfc1, bfc
                 nc.vector.quantize_mx(
                     out=w_codes[:, g, :].bitcast(FP8X4), scales=w_scales[:, g, :], in_=wg[:]
                 )
+            wg2 = wg_pool.tile([P, 4 * C], BF16, tag="wg", align_bytes=64)
+            wg2_v = wg2[:].rearrange("p (j o t) -> p j o t", j=NJ, o=P, t=4)
+            for j in range(NJ):
+                pk2 = ps_set.tile([P, 4, P], BF16, tag="set")
+                for t in range(4):
+                    c0 = j * C3 + 2 * C + t * P
+                    nc.tensor.transpose(pk2[:, t, :], w1_sb[:, c0 : c0 + P], ident_bf[:])
+                nc.vector.tensor_copy(out=wg2_v[:, j], in_=pk2[:].rearrange("p t o -> p o t"))
+            nc.vector.quantize_mx(
+                out=w_codes[:, 2, :].bitcast(FP8X4), scales=w_scales[:, 2, :], in_=wg2[:]
+            )
 
             ftT = setup.tile([P, NJ, P], BF16)
             pt = ps_set.tile([P, NJ, P], BF16, tag="set")
@@ -138,84 +168,108 @@ def tile_joint_module_pa_t_kernel(tc, fv, ft, W1, b1, g1, be1, m1, v1, Wfc1, bfc
             nc.tensor.matmul(pf[:], lhsT=ones_bf[:], rhs=bias_row[:], start=False, stop=True)
             nc.vector.tensor_scalar_add(out=gate[:], in0=pf[:], scalar1=1.0)
 
+            x2_words = x2[:].bitcast(F32).rearrange("b (t c r) -> b t r c", t=4, c=P, r=PX // 2)
+
+            def turn_in(c):
+                g2 = g2_pool.tile([P, B * 16], BF16, tag="g2", align_bytes=64)
+                g2_v = g2[:].rearrange("p (b h e t) -> p h b e t", b=B, h=2, e=2, t=4)
+                for h in range(2):
+                    pin = ps_acc.tile([P, 4, P], F32, tag="acc")
+                    for t in range(4):
+                        nc.tensor.transpose(pin[:, t, :], x2_words[:, t, 2 * c + h, :], ident_f[:])
+                    src = (
+                        pin[:]
+                        .rearrange("p t b -> p (t b)")
+                        .bitcast(BF16)
+                        .rearrange("p (t b e) -> p b e t", t=4, b=B, e=2)
+                    )
+                    if c % 2 == 0:
+                        nc.scalar.copy(out=g2_v[:, h], in_=src)
+                    else:
+                        nc.vector.tensor_copy(out=g2_v[:, h], in_=src)
+                return g2
+
+            def quantise2(c, g2):
+                for ch in range(NCH):
+                    nc.vector.quantize_mx(
+                        out=codes2[:, ch, c * QCOLS : (c + 1) * QCOLS].bitcast(FP8X4),
+                        scales=scales2[:, ch, c * QCOLS : (c + 1) * QCOLS],
+                        in_=g2[:, ch * 4 * QCOLS : (ch + 1) * 4 * QCOLS],
+                    )
+
+            prev = None
+            for c in range(NQ + 1):
+                cur = turn_in(c) if c < NQ else None
+                if c >= 1:
+                    quantise2(c - 1, prev)
+                prev = cur
+
+        with tc.tile_pool(name="ypool", bufs=1) as y_pool, tc.tile_pool(name="tmp", bufs=3) as tmp_pool:
+            y = y_pool.tile([P, NJ, PX, B], F32)
+
             state = {}
 
-            def load_and_group(ch, h, nb, g):
-                b0 = ch * CB + h * HB
-                if h == 0 and g == 0:
-                    codes = code_pool.tile([P, NG, COLS], U32, align_bytes=64)
-                    scales = code_pool.tile([P, NG, COLS], U8, align_bytes=64)
+            def group_up(ch, g):
+                if g == 0:
+                    codes = code_pool.tile([P, 2, COLS], U32, align_bytes=64)
+                    scales = code_pool.tile([P, 2, COLS], U8, align_bytes=64)
                     state[ch] = (codes, scales)
-                raw = raw_pool.tile([P, nb, 4, PX], BF16, tag="raw")
-                nc.sync.dma_start(
-                    out=raw[:].rearrange("p b t x -> p b (t x)"),
-                    in_=fv[b0 : b0 + nb, g * C : (g + 1) * C].rearrange(
-                        "b (p t) h w -> p b (t h w)", t=4
-                    ),
-                )
-                grp = grp_pool.tile([P, 4 * nb * PX], BF16, tag="grp", align_bytes=64)
-                na = 4 * nb * XA
+                grp = grp_pool.tile([P, 4 * COLS], BF16, tag="grp", align_bytes=64)
                 nc.vector.tensor_copy(
-                    out=grp[:, 0:na].rearrange("p (b c i t) -> p b c t i", b=nb, c=XA // 4, i=4, t=4),
-                    in_=raw[:, :, :, 0:XA].rearrange("p b t (c i) -> p b c t i", i=4),
-                )
-                nc.scalar.copy(
-                    out=grp[:, na : 4 * nb * PX].rearrange("p (b i t) -> p b t i", b=nb, i=XB, t=4),
-                    in_=raw[:, :, :, XA:PX],
+                    out=grp[:].rearrange("p (c b i t) -> p b c t i", c=NQ, b=CB, i=4, t=4),
+                    in_=raws[ch][:, g].rearrange("p b t (c i) -> p b c t i", i=4),
                 )
                 return grp
 
-            def quantise(ch, h, nb, g, grp):
+            def quantise(ch, g, grp):
                 codes, scales = state[ch]
-                na = 4 * nb * XA
-                lo, hi = h * HB * XA, (h * HB + nb) * XA
+                cut = 2 * WIDE
                 nc.vector.quantize_mx(
-                    out=codes[:, g, lo:hi].bitcast(FP8X4), scales=scales[:, g, lo:hi], in_=grp[:, 0:na]
+                    out=codes[:, g, 0:cut].bitcast(FP8X4), scales=scales[:, g, 0:cut], in_=grp[:, 0 : 4 * cut]
                 )
-                lo, hi = CA + h * HB * XB, CA + (h * HB + nb) * XB
                 nc.vector.quantize_mx(
-                    out=codes[:, g, lo:hi].bitcast(FP8X4),
-                    scales=scales[:, g, lo:hi],
-                    in_=grp[:, na : 4 * nb * PX],
+                    out=codes[:, g, cut:COLS].bitcast(FP8X4),
+                    scales=scales[:, g, cut:COLS],
+                    in_=grp[:, 4 * cut : 4 * COLS],
                 )
 
-            def mx_pass(acc, j, g, ch, lo, hi):
+            def group(acc, j, ch, lo, hi):
                 codes, scales = state[ch]
-                nc.tensor.matmul_mx(
-                    out=acc,
-                    lhsT=w_codes[:, g, j * P : (j + 1) * P].bitcast(FP8X4),
-                    lhsT_scale=w_scales[:, g, j * P : (j + 1) * P],
-                    rhs=codes[:, g, lo:hi].bitcast(FP8X4),
-                    rhs_scale=scales[:, g, lo:hi],
-                    start=(g == 0),
-                    stop=(g == NG - 1),
-                )
+                for n, g in enumerate(G_ORDER):
+                    if g == 2:
+                        rhs, rhs_scale = codes2[:, ch, lo:hi], scales2[:, ch, lo:hi]
+                    else:
+                        rhs, rhs_scale = codes[:, g, lo:hi], scales[:, g, lo:hi]
+                    nc.tensor.matmul_mx(
+                        out=acc,
+                        lhsT=w_codes[:, g, j * P : (j + 1) * P].bitcast(FP8X4),
+                        lhsT_scale=w_scales[:, g, j * P : (j + 1) * P],
+                        rhs=rhs.bitcast(FP8X4),
+                        rhs_scale=rhs_scale,
+                        start=(n == 0),
+                        stop=(n == NG - 1),
+                    )
 
-            def wide_out(acc, j, ch, s):
-                b0 = ch * CB + s * HB
+            def wide(j, ch, s):
+                b0 = ch * CB
+                acc = ps_acc.tile([P, WIDE], F32, tag="acc")
+                group(acc[:], j, ch, s * WIDE, (s + 1) * WIDE)
                 nc.scalar.activation(
-                    out=y[:, j, 0:XA, b0 : b0 + HB],
-                    in_=acc[:].rearrange("o (b x) -> o x b", x=XA),
+                    out=y[:, j, 16 * s : 16 * (s + 1), b0 : b0 + CB].rearrange("o (c i) b -> o c i b", i=4),
+                    in_=acc[:].rearrange("o (c b i) -> o c i b", c=4, b=CB, i=4),
                     func=ACT.Identity,
                     bias=bn_shift[:, j : j + 1],
                     scale=bn_scale[:, j : j + 1],
                 )
 
-            def wide(j, ch, s):
-                acc = ps_acc.tile([P, HB * XA], F32, tag="acc")
-                for g in range(NG):
-                    mx_pass(acc[:], j, g, ch, s * HB * XA, (s + 1) * HB * XA)
-                wide_out(acc, j, ch, s)
-
-            def narrow(j, ch, on_vector):
+            def narrow(j, ch, use_vector):
                 b0 = ch * CB
-                nar = ps_nar.tile([P, CB * XB], F32, tag="nar")
-                for g in range(NG):
-                    mx_pass(nar[:], j, g, ch, CA, COLS)
-                if on_vector:
+                nar = ps_nar.tile([P, QCOLS], F32, tag="nar")
+                group(nar[:], j, ch, 2 * WIDE, COLS)
+                if use_vector:
                     nc.vector.tensor_scalar(
-                        out=y[:, j, XA:PX, b0 : b0 + CB],
-                        in0=nar[:].rearrange("o (b x) -> o x b", x=XB),
+                        out=y[:, j, 32:PX, b0 : b0 + CB],
+                        in0=nar[:].rearrange("o (b i) -> o i b", i=4),
                         scalar1=bn_scale[:, j : j + 1],
                         scalar2=bn_shift[:, j : j + 1],
                         op0=ALU.mult,
@@ -223,59 +277,38 @@ def tile_joint_module_pa_t_kernel(tc, fv, ft, W1, b1, g1, be1, m1, v1, Wfc1, bfc
                     )
                 else:
                     nc.scalar.activation(
-                        out=y[:, j, XA:PX, b0 : b0 + CB],
-                        in_=nar[:].rearrange("o (b x) -> o x b", x=XB),
+                        out=y[:, j, 32:PX, b0 : b0 + CB],
+                        in_=nar[:].rearrange("o (b i) -> o i b", i=4),
                         func=ACT.Identity,
                         bias=bn_shift[:, j : j + 1],
                         scale=bn_scale[:, j : j + 1],
                     )
 
-            LAST = NCH - 1
-            open_acc = {}
-
-            def after(ch, h, nb, g):
-                if ch < LAST:
-                    if g == NG - 1:
-                        for j in range(NJ):
-                            wide(j, ch, 0)
-                            wide(j, ch, 1)
-                            narrow(j, ch, False)
-                elif h == 0:
-                    if g == NG - 1:
-                        for j in range(NJ):
-                            wide(j, ch, 0)
-                else:
-                    for j in J_ORDER:
-                        if g == 0:
-                            acc = ps_acc.tile([P, HB * XA], F32, tag="acc")
-                            open_acc[j] = acc
-                        mx_pass(open_acc[j][:], j, g, ch, HB * XA, 2 * HB * XA)
-                        if g == NG - 1:
-                            wide_out(open_acc[j], j, ch, 1)
-                            narrow(j, ch, True)
-
-            plan = [(ch, 0, CB, g) for ch in range(LAST) for g in range(NG)]
-            plan += [(LAST, h, HB, g) for h in range(2) for g in range(NG)]
+            plan = [(ch, g) for ch in range(NCH) for g in range(2)]
             last = None
             for n in range(len(plan) + 1):
-                grp = load_and_group(*plan[n]) if n < len(plan) else None
+                grp = group_up(*plan[n]) if n < len(plan) else None
                 if n >= 1:
-                    quantise(*plan[n - 1], last)
-                    after(*plan[n - 1])
+                    ch, g = plan[n - 1]
+                    quantise(ch, g, last)
+                    if g == 1:
+                        if ch == 0:
+                            load_chunk(3)
+                        for j in J_ORDER:
+                            wide(j, ch, 0)
+                            wide(j, ch, 1)
+                            narrow(j, ch, ch == NCH - 1)
                 last = grp
 
-        with tc.tile_pool(name="ost", bufs=4) as ost_pool, tc.tile_pool(name="tmp", bufs=3) as tmp_pool:
             osts = {}
 
             def turn(pool, tag, j, q):
                 if q == 0:
-                    ost = ost_pool.tile([P, P, PX], F32, tag="ost")
+                    ost = big_pool.tile([P, P, PX], F32, tag="big")
                     osts[j] = ost
                 tr = pool.tile([P, 4, P], F32, tag=tag)
                 for x in range(4):
                     nc.tensor.transpose(tr[:, x, :], y[:, j, 4 * q + x, :], ident_f[:])
-                idle = ps_nar.tile([P, KEEP_N], F32, tag="nar")
-                nc.tensor.matmul(idle[:], lhsT=ident_f[:], rhs=y[:, j, 4 * q, 0:KEEP_N], start=True, stop=True)
                 return tr
 
             def store(j):

@@ -183,10 +183,7 @@ def tile_joint_module_pa_t_kernel(tc, fv, ft, W1, b1, g1, be1, m1, v1, Wfc1, bfc
                         .bitcast(BF16)
                         .rearrange("p (t b e) -> p b e t", t=4, b=B, e=2)
                     )
-                    if c % 2 == 0:
-                        nc.scalar.copy(out=g2_v[:, h], in_=src)
-                    else:
-                        nc.vector.tensor_copy(out=g2_v[:, h], in_=src)
+                    nc.scalar.copy(out=g2_v[:, h], in_=src)
                 return g2
 
             def quantise2(c, g2):
@@ -255,8 +252,8 @@ def tile_joint_module_pa_t_kernel(tc, fv, ft, W1, b1, g1, be1, m1, v1, Wfc1, bfc
                 acc = ps_acc.tile([P, WIDE], F32, tag="acc")
                 group(acc[:], j, ch, s * WIDE, (s + 1) * WIDE)
                 nc.scalar.activation(
-                    out=y[:, j, 16 * s : 16 * (s + 1), b0 : b0 + CB].rearrange("o (c i) b -> o c i b", i=4),
-                    in_=acc[:].rearrange("o (c b i) -> o c i b", c=4, b=CB, i=4),
+                    out=y[:, j, 16 * s : 16 * (s + 1), b0 : b0 + CB].rearrange("o (c i) b -> o c b i", i=4),
+                    in_=acc[:].rearrange("o (c b i) -> o c b i", c=4, b=CB, i=4),
                     func=ACT.Identity,
                     bias=bn_shift[:, j : j + 1],
                     scale=bn_scale[:, j : j + 1],
@@ -268,8 +265,8 @@ def tile_joint_module_pa_t_kernel(tc, fv, ft, W1, b1, g1, be1, m1, v1, Wfc1, bfc
                 group(nar[:], j, ch, 2 * WIDE, COLS)
                 if use_vector:
                     nc.vector.tensor_scalar(
-                        out=y[:, j, 32:PX, b0 : b0 + CB],
-                        in0=nar[:].rearrange("o (b i) -> o i b", i=4),
+                        out=y[:, j, 32:PX, b0 : b0 + CB].rearrange("o i b -> o b i"),
+                        in0=nar[:].rearrange("o (b i) -> o b i", i=4),
                         scalar1=bn_scale[:, j : j + 1],
                         scalar2=bn_shift[:, j : j + 1],
                         op0=ALU.mult,
@@ -277,8 +274,8 @@ def tile_joint_module_pa_t_kernel(tc, fv, ft, W1, b1, g1, be1, m1, v1, Wfc1, bfc
                     )
                 else:
                     nc.scalar.activation(
-                        out=y[:, j, 32:PX, b0 : b0 + CB],
-                        in_=nar[:].rearrange("o (b i) -> o i b", i=4),
+                        out=y[:, j, 32:PX, b0 : b0 + CB].rearrange("o i b -> o b i"),
+                        in_=nar[:].rearrange("o (b i) -> o b i", i=4),
                         func=ACT.Identity,
                         bias=bn_shift[:, j : j + 1],
                         scale=bn_scale[:, j : j + 1],

@@ -19,10 +19,12 @@ NG = 3
 NJ = 4
 CB = 32
 NCH = B // CB
+LAST = NCH - 1
+NR = PX // 2
 NQ = PX // 4
 COLS = CB * PX
-QCOLS = CB * 4
-WIDE = 4 * QCOLS
+RCOLS = CB * 2
+WIDE = 8 * RCOLS
 J_ORDER = (0, 3, 1, 2)
 J_VECTOR = (0, 1, 2)
 G_ORDER = (2, 0, 1)
@@ -34,10 +36,9 @@ def tile_joint_module_pa_t_kernel(tc, fv, ft, W1, b1, g1, be1, m1, v1, Wfc1, bfc
     nc = tc.nc
     with ExitStack() as keep_ctx:
         keep = keep_ctx.enter_context(tc.tile_pool(name="keep", bufs=1))
-        ps_acc = keep_ctx.enter_context(tc.psum_pool(name="ps_acc", bufs=4))
-        ps_nar = keep_ctx.enter_context(tc.psum_pool(name="ps_nar", bufs=2))
-        ps_set = keep_ctx.enter_context(tc.psum_pool(name="ps_set", bufs=2))
+        psum = keep_ctx.enter_context(tc.psum_pool(name="psum", bufs=8))
         big_pool = keep_ctx.enter_context(tc.tile_pool(name="big", bufs=3))
+        x2_pool = keep_ctx.enter_context(tc.tile_pool(name="x2", bufs=2))
         grp_pool = keep_ctx.enter_context(tc.tile_pool(name="grp", bufs=3))
         code_pool = keep_ctx.enter_context(tc.tile_pool(name="code", bufs=2))
 
@@ -50,15 +51,24 @@ def tile_joint_module_pa_t_kernel(tc, fv, ft, W1, b1, g1, be1, m1, v1, Wfc1, bfc
 
         w_codes = keep.tile([P, NG, C], U32, align_bytes=64)
         w_scales = keep.tile([P, NG, C], U8, align_bytes=64)
-        codes2 = keep.tile([P, NCH, COLS], U32, align_bytes=64)
-        scales2 = keep.tile([P, NCH, COLS], U8, align_bytes=64)
         gate = keep.tile([P, C], F32)
         bn_scale = keep.tile([P, NJ], F32)
         bn_shift = keep.tile([P, NJ], F32)
 
         raws = {}
+        x2s = {}
 
-        def load_chunk(ch):
+        def load_x2(ch):
+            b0 = ch * CB
+            x2c = x2_pool.tile([P, P * PX], BF16, tag="x2c")
+            for t in range(4):
+                nc.sync.dma_start(
+                    out=x2c[t : P : 4, :],
+                    in_=fv[b0 : b0 + CB, 2 * C + t * P : 2 * C + (t + 1) * P].rearrange("b c h w -> b (c h w)"),
+                )
+            x2s[ch] = x2c
+
+        def load_raw(ch):
             b0 = ch * CB
             raw = big_pool.tile([P, 2, CB, 4, PX], BF16, tag="big")
             for g in range(2):
@@ -73,7 +83,6 @@ def tile_joint_module_pa_t_kernel(tc, fv, ft, W1, b1, g1, be1, m1, v1, Wfc1, bfc
         with ExitStack() as a_ctx:
             setup = a_ctx.enter_context(tc.tile_pool(name="setup", bufs=1))
             wg_pool = a_ctx.enter_context(tc.tile_pool(name="wg", bufs=2))
-            g2_pool = a_ctx.enter_context(tc.tile_pool(name="g2", bufs=3))
 
             w1_sb = setup.tile([P, NJ * C3], BF16)
             nc.sync.dma_start(
@@ -94,16 +103,11 @@ def tile_joint_module_pa_t_kernel(tc, fv, ft, W1, b1, g1, be1, m1, v1, Wfc1, bfc
             nc.scalar.dma_start(out=ft_sb[:], in_=ft)
             wfc_sb = setup.tile([P, NJ, C], BF16)
             nc.scalar.dma_start(out=wfc_sb[:], in_=Wfc1.rearrange("(j o) k -> o j k", j=NJ))
-            x2 = setup.tile([P, C * PX], BF16)
-            for t in range(4):
-                nc.sync.dma_start(
-                    out=x2[:, t * P * PX : (t + 1) * P * PX],
-                    in_=fv[:, 2 * C + t * P : 2 * C + (t + 1) * P].rearrange("b c h w -> b (c h w)"),
-                )
-            for ch in range(3):
-                load_chunk(ch)
+            for ch in range(2):
+                load_x2(ch)
+                load_raw(ch)
 
-            pv = ps_set.tile([P, P], BF16, tag="set")
+            pv = psum.tile([P, P], BF16, tag="bank")
             nc.tensor.transpose(pv[:], vec_rows[:], ident_bf[:])
             vecs = setup.tile([P, 5 * NJ], F32)
             nc.vector.tensor_copy(out=vecs[:], in_=pv[:, 0 : 5 * NJ])
@@ -126,7 +130,7 @@ def tile_joint_module_pa_t_kernel(tc, fv, ft, W1, b1, g1, be1, m1, v1, Wfc1, bfc
                 wg = wg_pool.tile([P, 4 * C], BF16, tag="wg", align_bytes=64)
                 wg_words = wg[:].bitcast(F32).rearrange("p (j o u) -> p j o u", j=NJ, o=P, u=2)
                 for jp in range(NJ // 2):
-                    pw = ps_set.tile([P, 2, 2, P], F32, tag="set")
+                    pw = psum.tile([P, 2, 2, P], F32, tag="bank")
                     for jj in range(2):
                         for u in range(2):
                             nc.tensor.transpose(
@@ -142,7 +146,7 @@ def tile_joint_module_pa_t_kernel(tc, fv, ft, W1, b1, g1, be1, m1, v1, Wfc1, bfc
             wg2 = wg_pool.tile([P, 4 * C], BF16, tag="wg", align_bytes=64)
             wg2_v = wg2[:].rearrange("p (j o t) -> p j o t", j=NJ, o=P, t=4)
             for j in range(NJ):
-                pk2 = ps_set.tile([P, 4, P], BF16, tag="set")
+                pk2 = psum.tile([P, 4, P], BF16, tag="bank")
                 for t in range(4):
                     c0 = j * C3 + 2 * C + t * P
                     nc.tensor.transpose(pk2[:, t, :], w1_sb[:, c0 : c0 + P], ident_bf[:])
@@ -152,121 +156,97 @@ def tile_joint_module_pa_t_kernel(tc, fv, ft, W1, b1, g1, be1, m1, v1, Wfc1, bfc
             )
 
             ftT = setup.tile([P, NJ, P], BF16)
-            pt = ps_set.tile([P, NJ, P], BF16, tag="set")
+            pt = psum.tile([P, NJ, P], BF16, tag="bank")
             for kc in range(NJ):
                 nc.tensor.transpose(pt[:, kc, :], ft_sb[:, kc * P : (kc + 1) * P], ident_bf[:])
             nc.vector.tensor_copy(out=ftT[:], in_=pt[:])
             wfcT = setup.tile([P, NJ, C], BF16)
             for kc in range(NJ):
-                pk = ps_set.tile([P, NJ, P], BF16, tag="set")
+                pk = psum.tile([P, NJ, P], BF16, tag="bank")
                 for j in range(NJ):
                     nc.tensor.transpose(pk[:, j, :], wfc_sb[:, j, kc * P : (kc + 1) * P], ident_bf[:])
                 nc.scalar.copy(out=wfcT[:, kc, :], in_=pk[:].rearrange("p j o -> p (j o)"))
-            pf = ps_set.tile([P, C], F32, tag="set")
+            pf = psum.tile([P, C], F32, tag="bank")
             for kc in range(NJ):
                 nc.tensor.matmul(pf[:], lhsT=ftT[:, kc, :], rhs=wfcT[:, kc, :], start=(kc == 0), stop=False)
             nc.tensor.matmul(pf[:], lhsT=ones_bf[:], rhs=bias_row[:], start=False, stop=True)
             nc.vector.tensor_scalar_add(out=gate[:], in0=pf[:], scalar1=1.0)
 
-            x2_words = x2[:].bitcast(F32).rearrange("b (t c r) -> b t r c", t=4, c=P, r=PX // 2)
-
-            def turn_in(c):
-                g2 = g2_pool.tile([P, B * 16], BF16, tag="g2", align_bytes=64)
-                g2_v = g2[:].rearrange("p (b h e t) -> p h b e t", b=B, h=2, e=2, t=4)
-                for h in range(2):
-                    pin = ps_acc.tile([P, 4, P], F32, tag="acc")
-                    for t in range(4):
-                        nc.tensor.transpose(pin[:, t, :], x2_words[:, t, 2 * c + h, :], ident_f[:])
-                    src = (
-                        pin[:]
-                        .rearrange("p t b -> p (t b)")
-                        .bitcast(BF16)
-                        .rearrange("p (t b e) -> p b e t", t=4, b=B, e=2)
-                    )
-                    nc.scalar.copy(out=g2_v[:, h], in_=src)
-                return g2
-
-            def quantise2(c, g2):
-                for ch in range(NCH):
-                    nc.vector.quantize_mx(
-                        out=codes2[:, ch, c * QCOLS : (c + 1) * QCOLS].bitcast(FP8X4),
-                        scales=scales2[:, ch, c * QCOLS : (c + 1) * QCOLS],
-                        in_=g2[:, ch * 4 * QCOLS : (ch + 1) * 4 * QCOLS],
-                    )
-
-            prev = None
-            for c in range(NQ + 1):
-                cur = turn_in(c) if c < NQ else None
-                if c >= 1:
-                    quantise2(c - 1, prev)
-                prev = cur
-
-        with tc.tile_pool(name="ypool", bufs=1) as y_pool, tc.tile_pool(name="tmp", bufs=3) as tmp_pool:
+        with tc.tile_pool(name="ypool", bufs=1) as y_pool, tc.tile_pool(name="tmp", bufs=3) as tmp_pool, tc.manual_schedule():
             y = y_pool.tile([P, NJ, PX, B], F32)
 
             state = {}
+            grps = {}
+            SLICES = ((0, 8), (8, 16), (16, NR))
 
-            def group_up(ch, g):
-                if g == 0:
-                    codes = code_pool.tile([P, 2, COLS], U32, align_bytes=64)
-                    scales = code_pool.tile([P, 2, COLS], U8, align_bytes=64)
-                    state[ch] = (codes, scales)
+            def turn_in(ch):
+                codes = code_pool.tile([P, NG, COLS], U32, align_bytes=64)
+                scales = code_pool.tile([P, NG, COLS], U8, align_bytes=64)
+                state[ch] = (codes, scales)
                 grp = grp_pool.tile([P, 4 * COLS], BF16, tag="grp", align_bytes=64)
-                nc.vector.tensor_copy(
-                    out=grp[:].rearrange("p (c b i t) -> p b c t i", c=NQ, b=CB, i=4, t=4),
-                    in_=raws[ch][:, g].rearrange("p b t (c i) -> p b c t i", i=4),
-                )
-                return grp
+                grps[(ch, 2)] = grp
+                words = x2s[ch][:].bitcast(F32).rearrange("p (c r) -> p r c", r=NR)
+                for r0 in range(0, NR, 4):
+                    nr = min(4, NR - r0)
+                    pin = psum.tile([P, 4, P], F32, tag="bank")
+                    for k in range(nr):
+                        nc.tensor.transpose(pin[:, k, :], words[:, r0 + k, :], ident_f[:])
+                    nc.scalar.copy(
+                        out=grp[:, r0 * 4 * RCOLS : (r0 + nr) * 4 * RCOLS].rearrange(
+                            "p (q e t) -> p q e t", e=2, t=4
+                        ),
+                        in_=pin[:, 0:nr, :]
+                        .rearrange("p r w -> p (r w)")
+                        .bitcast(BF16)
+                        .rearrange("p (q t e) -> p q e t", t=4, e=2),
+                    )
+                if ch + 2 < NCH:
+                    load_x2(ch + 2)
 
-            def quantise(ch, g, grp):
-                codes, scales = state[ch]
-                cut = 2 * WIDE
-                nc.vector.quantize_mx(
-                    out=codes[:, g, 0:cut].bitcast(FP8X4), scales=scales[:, g, 0:cut], in_=grp[:, 0 : 4 * cut]
-                )
-                nc.vector.quantize_mx(
-                    out=codes[:, g, cut:COLS].bitcast(FP8X4),
-                    scales=scales[:, g, cut:COLS],
-                    in_=grp[:, 4 * cut : 4 * COLS],
-                )
-
-            def group(acc, j, ch, lo, hi):
-                codes, scales = state[ch]
-                for n, g in enumerate(G_ORDER):
-                    if g == 2:
-                        rhs, rhs_scale = codes2[:, ch, lo:hi], scales2[:, ch, lo:hi]
-                    else:
-                        rhs, rhs_scale = codes[:, g, lo:hi], scales[:, g, lo:hi]
-                    nc.tensor.matmul_mx(
-                        out=acc,
-                        lhsT=w_codes[:, g, j * P : (j + 1) * P].bitcast(FP8X4),
-                        lhsT_scale=w_scales[:, g, j * P : (j + 1) * P],
-                        rhs=rhs.bitcast(FP8X4),
-                        rhs_scale=rhs_scale,
-                        start=(n == 0),
-                        stop=(n == NG - 1),
+            def group_up(ch, g, parts):
+                if (ch, g) not in grps:
+                    grp = grp_pool.tile([P, 4 * COLS], BF16, tag="grp", align_bytes=64)
+                    grps[(ch, g)] = grp
+                for r0, r1 in parts:
+                    nc.vector.tensor_copy(
+                        out=grps[(ch, g)][:, r0 * 4 * RCOLS : r1 * 4 * RCOLS].rearrange(
+                            "p (r b e t) -> p b r t e", r=r1 - r0, b=CB, e=2, t=4
+                        ),
+                        in_=raws[ch][:, g, :, :, 2 * r0 : 2 * r1].rearrange("p b t (r e) -> p b r t e", e=2),
                     )
 
-            def wide(j, ch, s):
-                b0 = ch * CB
-                acc = ps_acc.tile([P, WIDE], F32, tag="acc")
-                group(acc[:], j, ch, s * WIDE, (s + 1) * WIDE)
-                nc.scalar.activation(
-                    out=y[:, j, 16 * s : 16 * (s + 1), b0 : b0 + CB].rearrange("o (c i) b -> o c b i", i=4),
-                    in_=acc[:].rearrange("o (c b i) -> o c b i", c=4, b=CB, i=4),
-                    func=ACT.Identity,
-                    bias=bn_shift[:, j : j + 1],
-                    scale=bn_scale[:, j : j + 1],
+            def quantise(ch, g, parts):
+                codes, scales = state[ch]
+                for r0, r1 in parts:
+                    lo, hi = r0 * RCOLS, r1 * RCOLS
+                    nc.vector.quantize_mx(
+                        out=codes[:, g, lo:hi].bitcast(FP8X4),
+                        scales=scales[:, g, lo:hi],
+                        in_=grps[(ch, g)][:, 4 * lo : 4 * hi],
+                    )
+
+            def mx_pass(acc, j, g, ch, part):
+                codes, scales = state[ch]
+                lo, hi = part[0] * RCOLS, part[1] * RCOLS
+                nc.tensor.matmul_mx(
+                    out=acc[:, 0 : hi - lo],
+                    lhsT=w_codes[:, g, j * P : (j + 1) * P].bitcast(FP8X4),
+                    lhsT_scale=w_scales[:, g, j * P : (j + 1) * P],
+                    rhs=codes[:, g, lo:hi].bitcast(FP8X4),
+                    rhs_scale=scales[:, g, lo:hi],
+                    start=(g == G_ORDER[0]),
+                    stop=(g == G_ORDER[-1]),
                 )
 
-            def narrow(j, ch, use_vector):
+            def leave(acc, j, ch, part, use_vector):
+                r0, r1 = part
                 b0 = ch * CB
-                nar = ps_nar.tile([P, QCOLS], F32, tag="nar")
-                group(nar[:], j, ch, 2 * WIDE, COLS)
+                dst = y[:, j, 2 * r0 : 2 * r1, b0 : b0 + CB].rearrange("o (r e) b -> o r b e", e=2)
+                src = acc[:, 0 : (r1 - r0) * RCOLS].rearrange("o (r b e) -> o r b e", r=r1 - r0, b=CB, e=2)
                 if use_vector:
                     nc.vector.tensor_scalar(
-                        out=y[:, j, 32:PX, b0 : b0 + CB].rearrange("o i b -> o b i"),
-                        in0=nar[:].rearrange("o (b i) -> o b i", i=4),
+                        out=dst,
+                        in0=src,
                         scalar1=bn_scale[:, j : j + 1],
                         scalar2=bn_shift[:, j : j + 1],
                         op0=ALU.mult,
@@ -274,36 +254,62 @@ def tile_joint_module_pa_t_kernel(tc, fv, ft, W1, b1, g1, be1, m1, v1, Wfc1, bfc
                     )
                 else:
                     nc.scalar.activation(
-                        out=y[:, j, 32:PX, b0 : b0 + CB].rearrange("o i b -> o b i"),
-                        in_=nar[:].rearrange("o (b i) -> o b i", i=4),
+                        out=dst,
+                        in_=src,
                         func=ACT.Identity,
                         bias=bn_shift[:, j : j + 1],
                         scale=bn_scale[:, j : j + 1],
                     )
 
-            plan = [(ch, g) for ch in range(NCH) for g in range(2)]
-            last = None
-            for n in range(len(plan) + 1):
-                grp = group_up(*plan[n]) if n < len(plan) else None
-                if n >= 1:
-                    ch, g = plan[n - 1]
-                    quantise(ch, g, last)
-                    if g == 1:
-                        if ch == 0:
-                            load_chunk(3)
-                        for j in J_ORDER:
-                            wide(j, ch, 0)
-                            wide(j, ch, 1)
-                            narrow(j, ch, ch == NCH - 1)
-                last = grp
+            def whole_group(j, ch, part, use_vector):
+                acc = psum.tile([P, WIDE], F32, tag="bank")
+                for g in G_ORDER:
+                    mx_pass(acc, j, g, ch, part)
+                leave(acc, j, ch, part, use_vector)
+
+            ALL = ((0, 16), (16, NR))
+            open_acc = {}
+
+            def finish(j):
+                for part in SLICES[0:2]:
+                    mx_pass(open_acc[(j, part)], j, 1, LAST, part)
+                    leave(open_acc[(j, part)], j, LAST, part, False)
+                whole_group(j, LAST, SLICES[2], True)
+
+            turn_in(0)
+            for ch in range(NCH):
+                group_up(ch, 0, ((0, NR),))
+                quantise(ch, 2, ALL)
+                if ch + 1 < NCH:
+                    turn_in(ch + 1)
+                quantise(ch, 0, ALL)
+                if ch == LAST:
+                    for j in J_ORDER:
+                        for part in SLICES[0:2]:
+                            acc = psum.tile([P, WIDE], F32, tag="bank")
+                            open_acc[(j, part)] = acc
+                            mx_pass(acc, j, 2, ch, part)
+                            mx_pass(acc, j, 0, ch, part)
+                group_up(ch, 1, SLICES[0:2])
+                quantise(ch, 1, SLICES[0:1])
+                group_up(ch, 1, SLICES[2:3])
+                quantise(ch, 1, SLICES[1:3])
+                if ch + 2 < NCH:
+                    load_raw(ch + 2)
+                if ch < LAST:
+                    for part in SLICES:
+                        for j in range(NJ):
+                            whole_group(j, ch, part, False)
+            finish(J_ORDER[0])
+            finish(J_ORDER[1])
 
             osts = {}
 
-            def turn(pool, tag, j, q):
+            def turn(j, q):
                 if q == 0:
                     ost = big_pool.tile([P, P, PX], F32, tag="big")
                     osts[j] = ost
-                tr = pool.tile([P, 4, P], F32, tag=tag)
+                tr = psum.tile([P, 4, P], F32, tag="bank")
                 for x in range(4):
                     nc.tensor.transpose(tr[:, x, :], y[:, j, 4 * q + x, :], ident_f[:])
                 return tr
@@ -318,7 +324,7 @@ def tile_joint_module_pa_t_kernel(tc, fv, ft, W1, b1, g1, be1, m1, v1, Wfc1, bfc
                 return gate[:, j * P : (j + 1) * P].unsqueeze(2).to_broadcast([P, P, 4])
 
             def on_vector(j, q):
-                tr = turn(ps_acc, "acc", j, q)
+                tr = turn(j, q)
                 nc.vector.scalar_tensor_tensor(
                     out=osts[j][:, :, 4 * q : 4 * q + 4],
                     in0=tr[:].rearrange("b x o -> b o x"),
@@ -331,7 +337,7 @@ def tile_joint_module_pa_t_kernel(tc, fv, ft, W1, b1, g1, be1, m1, v1, Wfc1, bfc
                     store(j)
 
             def on_scalar_gpsimd(j, q):
-                tr = turn(ps_set, "set", j, q)
+                tr = turn(j, q)
                 tmp = tmp_pool.tile([P, P, 4], F32, tag="tmp")
                 nc.scalar.activation(out=tmp[:], in_=tr[:].rearrange("b x o -> b o x"), func=ACT.Relu)
                 nc.gpsimd.tensor_tensor(
@@ -341,6 +347,10 @@ def tile_joint_module_pa_t_kernel(tc, fv, ft, W1, b1, g1, be1, m1, v1, Wfc1, bfc
                     store(j)
 
             for i in range(3 * NQ):
-                if i % 3 == 0:
-                    on_scalar_gpsimd(J_ORDER[1], i // 3)
+                if i % 2 == 0 and i < 2 * NQ:
+                    on_scalar_gpsimd(J_ORDER[1], i // 2)
                 on_vector(J_VECTOR[i // NQ], i % NQ)
+                if i == 1:
+                    finish(J_ORDER[2])
+                if i == 5:
+                    finish(J_ORDER[3])

@@ -282,14 +282,17 @@ def tile_joint_module_pa_t_kernel(tc, fv, ft, W1, b1, g1, be1, m1, v1, Wfc1, bfc
                 quantise(ch, 2, ALL)
                 if ch + 1 < NCH:
                     turn_in(ch + 1)
-                quantise(ch, 0, ALL)
-                if ch == LAST:
+                else:
                     for j in J_ORDER:
                         for part in SLICES[0:2]:
                             acc = psum.tile([P, WIDE], F32, tag="bank")
                             open_acc[(j, part)] = acc
                             mx_pass(acc, j, 2, ch, part)
-                            mx_pass(acc, j, 0, ch, part)
+                quantise(ch, 0, ALL)
+                if ch == LAST:
+                    for j in J_ORDER:
+                        for part in SLICES[0:2]:
+                            mx_pass(open_acc[(j, part)], j, 0, ch, part)
                 group_up(ch, 1, SLICES[0:2])
                 quantise(ch, 1, SLICES[0:1])
                 group_up(ch, 1, SLICES[2:3])
@@ -347,9 +350,9 @@ def tile_joint_module_pa_t_kernel(tc, fv, ft, W1, b1, g1, be1, m1, v1, Wfc1, bfc
                     store(j)
 
             for i in range(3 * NQ):
-                if i % 2 == 0 and i < 2 * NQ:
-                    on_scalar_gpsimd(J_ORDER[1], i // 2)
                 on_vector(J_VECTOR[i // NQ], i % NQ)
+                if i % 2 == 1 and i < 2 * NQ:
+                    on_scalar_gpsimd(J_ORDER[1], i // 2)
                 if i == 1:
                     finish(J_ORDER[2])
                 if i == 5:

@@ -19,234 +19,191 @@ NG = 3
 NJ = 4
 CB = 32
 NCH = B // CB
-LAST = NCH - 1
 NR = PX // 2
-NQ = PX // 4
 COLS = CB * PX
-RCOLS = CB * 2
-WIDE = 8 * RCOLS
-J_ORDER = (0, 3, 1, 2)
-J_VECTOR = (0, 1, 2)
-G_ORDER = (2, 0, 1)
+SLICES = ((0, 512), (512, 1024), (1024, COLS))
+SAMPLES = ((0, 14), (14, 28), (28, CB))
 
 FLOPS = 2 * C * C3 * B * PX + 2 * B * C * C
 
 
 def tile_joint_module_pa_t_kernel(tc, fv, ft, W1, b1, g1, be1, m1, v1, Wfc1, bfc1, out):
     nc = tc.nc
-    with ExitStack() as keep_ctx:
-        keep = keep_ctx.enter_context(tc.tile_pool(name="keep", bufs=1))
-        psum = keep_ctx.enter_context(tc.psum_pool(name="psum", bufs=8))
-        big_pool = keep_ctx.enter_context(tc.tile_pool(name="big", bufs=3))
-        x2_pool = keep_ctx.enter_context(tc.tile_pool(name="x2", bufs=2))
-        grp_pool = keep_ctx.enter_context(tc.tile_pool(name="grp", bufs=3))
-        code_pool = keep_ctx.enter_context(tc.tile_pool(name="code", bufs=2))
+    with ExitStack() as ctx:
+        keep = ctx.enter_context(tc.tile_pool(name="keep", bufs=1))
+        psum_t = ctx.enter_context(tc.psum_pool(name="psum_t", bufs=4))
+        psum_m = ctx.enter_context(tc.psum_pool(name="psum_m", bufs=4))
+        x2_pool = ctx.enter_context(tc.tile_pool(name="x2", bufs=2))
+        raw_pool = ctx.enter_context(tc.tile_pool(name="raw", bufs=2))
+        grp_pool = ctx.enter_context(tc.tile_pool(name="grp", bufs=4))
+        code_pool = ctx.enter_context(tc.tile_pool(name="code", bufs=2))
+        y_pool = ctx.enter_context(tc.tile_pool(name="y", bufs=1))
+        ost_pool = ctx.enter_context(tc.tile_pool(name="ost", bufs=2))
+        setup = ctx.enter_context(tc.tile_pool(name="setup", bufs=1))
+        wg_pool = ctx.enter_context(tc.tile_pool(name="wg", bufs=2))
+        ctx.enter_context(tc.manual_schedule())
 
         ident_bf = keep.tile([P, P], BF16)
         make_identity(nc, ident_bf[:])
         ident_f = keep.tile([P, P], F32)
         make_identity(nc, ident_f[:])
-        ones_bf = keep.tile([P, P], BF16)
-        nc.vector.memset(ones_bf[:], 1.0)
-
         w_codes = keep.tile([P, NG, C], U32, align_bytes=64)
         w_scales = keep.tile([P, NG, C], U8, align_bytes=64)
-        gate = keep.tile([P, C], F32)
+        gate = keep.tile([P, NJ, B], F32)
         bn_scale = keep.tile([P, NJ], F32)
         bn_shift = keep.tile([P, NJ], F32)
 
-        raws = {}
-        x2s = {}
+        x2s, raws, grps, codes_of = {}, {}, {}, {}
 
         def load_x2(ch):
             b0 = ch * CB
-            x2c = x2_pool.tile([P, P * PX], BF16, tag="x2c")
+            x2c = x2_pool.tile([P, 2, P * PX], BF16, tag="x2c")
             for t in range(4):
                 nc.sync.dma_start(
-                    out=x2c[t : P : 4, :],
-                    in_=fv[b0 : b0 + CB, 2 * C + t * P : 2 * C + (t + 1) * P].rearrange("b c h w -> b (c h w)"),
+                    out=x2c[t : P : 4],
+                    in_=fv[b0 : b0 + CB, C:]
+                    .rearrange("b (g q c) h w -> b g q (c h w)", g=2, q=4)[:, :, t],
                 )
             x2s[ch] = x2c
 
         def load_raw(ch):
             b0 = ch * CB
-            raw = big_pool.tile([P, 2, CB, 4, PX], BF16, tag="big")
-            for g in range(2):
-                nc.sync.dma_start(
-                    out=raw[:, g].rearrange("p b t x -> p b (t x)"),
-                    in_=fv[b0 : b0 + CB, g * C : (g + 1) * C].rearrange(
-                        "b (p t) h w -> p b (t h w)", t=4
-                    ),
-                )
+            raw = raw_pool.tile([P, CB, 4, PX], BF16, tag="raw")
+            nc.sync.dma_start(
+                out=raw[:].rearrange("p b t x -> p b (t x)"),
+                in_=fv[b0 : b0 + CB, 0:C].rearrange("b (p t) h w -> p b (t h w)", t=4),
+            )
             raws[ch] = raw
 
-        with ExitStack() as a_ctx:
-            setup = a_ctx.enter_context(tc.tile_pool(name="setup", bufs=1))
-            wg_pool = a_ctx.enter_context(tc.tile_pool(name="wg", bufs=2))
+        vec_rows = setup.tile([P, C], BF16)
+        nc.vector.memset(vec_rows[:], 0.0)
+        w1_sb = setup.tile([P, NJ * C3], BF16)
+        nc.sync.dma_start(out=w1_sb[:], in_=W1.rearrange("(o j) c -> o (j c)", j=NJ))
+        for i, vec in enumerate((b1, g1, be1, m1, v1, bfc1)):
+            nc.scalar.dma_start(out=vec_rows[i : i + 1, :], in_=vec.rearrange("(o c) -> o c", o=1))
+        load_x2(0)
+        load_raw(0)
+        ft_sb = setup.tile([P, C], BF16)
+        nc.sync.dma_start(out=ft_sb[:], in_=ft)
+        wfc_sb = setup.tile([P, NJ, C], BF16)
+        nc.sync.dma_start(out=wfc_sb[:], in_=Wfc1.rearrange("(o j) k -> o j k", j=NJ))
+        load_x2(1)
+        load_raw(1)
 
-            w1_sb = setup.tile([P, NJ * C3], BF16)
-            nc.sync.dma_start(
-                out=w1_sb[:].rearrange("o (j c) -> o j c", j=NJ),
-                in_=W1.rearrange("(j o) c -> o j c", j=NJ),
+        pv = psum_t.tile([P, NJ, P], BF16, tag="bank")
+        for j in range(NJ):
+            nc.tensor.transpose(pv[:, j, :], vec_rows[:, j : C : NJ], ident_bf[:])
+        vecs = setup.tile([P, 6, NJ], F32)
+        nc.vector.tensor_copy(out=vecs[:].rearrange("p i j -> p j i"), in_=pv[:, :, 0:6])
+        std = setup.tile([P, NJ], F32)
+        nc.vector.tensor_scalar_add(out=std[:], in0=vecs[:, 4], scalar1=EPS)
+        nc.scalar.sqrt(std[:], std[:])
+
+        w_words = w1_sb[:].bitcast(F32).rearrange("o (j g p u) -> o j g u p", j=NJ, g=NG, p=P, u=2)
+        wg = wg_pool.tile([P, 4 * C], BF16, tag="wg", align_bytes=64)
+        wg_words = wg[:].bitcast(F32).rearrange("p (j o u) -> p j o u", j=NJ, o=P, u=2)
+        for jp in range(NJ // 2):
+            pw = psum_m.tile([P, 2, 2, P], F32, tag="bank")
+            for jj in range(2):
+                for u in range(2):
+                    nc.tensor.transpose(pw[:, jj, u, :], w_words[:, 2 * jp + jj, 0, u, :], ident_f[:])
+            nc.vector.tensor_copy(
+                out=wg_words[:, 2 * jp : 2 * jp + 2], in_=pw[:].rearrange("p j u o -> p j o u")
             )
-            vec_rows = setup.tile([P, P], BF16)
-            nc.vector.memset(vec_rows[:], 0.0)
-            for i, vec in enumerate((b1, g1, be1, m1, v1)):
-                nc.scalar.dma_start(
-                    out=vec_rows[NJ * i : NJ * (i + 1), :],
-                    in_=vec.rearrange("(j c) -> j c", j=NJ),
-                )
-            bias_row = setup.tile([P, C], BF16)
-            nc.vector.memset(bias_row[:], 0.0)
-            nc.scalar.dma_start(out=bias_row[0:1, :], in_=bfc1.rearrange("(o c) -> o c", o=1))
-            ft_sb = setup.tile([P, C], BF16)
-            nc.scalar.dma_start(out=ft_sb[:], in_=ft)
-            wfc_sb = setup.tile([P, NJ, C], BF16)
-            nc.scalar.dma_start(out=wfc_sb[:], in_=Wfc1.rearrange("(j o) k -> o j k", j=NJ))
-            for ch in range(2):
-                load_x2(ch)
-                load_raw(ch)
-
-            pv = psum.tile([P, P], BF16, tag="bank")
-            nc.tensor.transpose(pv[:], vec_rows[:], ident_bf[:])
-            vecs = setup.tile([P, 5 * NJ], F32)
-            nc.vector.tensor_copy(out=vecs[:], in_=pv[:, 0 : 5 * NJ])
-            col = lambda i: vecs[:, NJ * i : NJ * (i + 1)]
-            std = setup.tile([P, NJ], F32)
-            nc.vector.tensor_scalar_add(out=std[:], in0=col(4), scalar1=EPS)
-            nc.scalar.sqrt(std[:], std[:])
-            rstd = setup.tile([P, NJ], F32)
-            nc.vector.reciprocal(rstd[:], std[:])
-            nc.vector.tensor_mul(out=bn_scale[:], in0=col(1), in1=rstd[:])
-            diff = setup.tile([P, NJ], F32)
-            nc.vector.tensor_sub(out=diff[:], in0=col(0), in1=col(3))
-            nc.vector.tensor_mul(out=diff[:], in0=diff[:], in1=bn_scale[:])
-            nc.vector.tensor_add(out=bn_shift[:], in0=diff[:], in1=col(2))
-
-            w_words = w1_sb[:].bitcast(F32).rearrange(
-                "o (j g p u) -> o j g u p", j=NJ, g=NG, p=P, u=2
-            )
-            for g in range(2):
-                wg = wg_pool.tile([P, 4 * C], BF16, tag="wg", align_bytes=64)
-                wg_words = wg[:].bitcast(F32).rearrange("p (j o u) -> p j o u", j=NJ, o=P, u=2)
-                for jp in range(NJ // 2):
-                    pw = psum.tile([P, 2, 2, P], F32, tag="bank")
-                    for jj in range(2):
-                        for u in range(2):
-                            nc.tensor.transpose(
-                                pw[:, jj, u, :], w_words[:, 2 * jp + jj, g, u, :], ident_f[:]
-                            )
-                    nc.vector.tensor_copy(
-                        out=wg_words[:, 2 * jp : 2 * jp + 2],
-                        in_=pw[:].rearrange("p j u o -> p j o u"),
-                    )
-                nc.vector.quantize_mx(
-                    out=w_codes[:, g, :].bitcast(FP8X4), scales=w_scales[:, g, :], in_=wg[:]
-                )
+        wgs = [wg]
+        for g in (1, 2):
             wg2 = wg_pool.tile([P, 4 * C], BF16, tag="wg", align_bytes=64)
             wg2_v = wg2[:].rearrange("p (j o t) -> p j o t", j=NJ, o=P, t=4)
             for j in range(NJ):
-                pk2 = psum.tile([P, 4, P], BF16, tag="bank")
+                pk2 = psum_m.tile([P, 4, P], BF16, tag="bank")
                 for t in range(4):
-                    c0 = j * C3 + 2 * C + t * P
+                    c0 = j * C3 + g * C + t * P
                     nc.tensor.transpose(pk2[:, t, :], w1_sb[:, c0 : c0 + P], ident_bf[:])
                 nc.vector.tensor_copy(out=wg2_v[:, j], in_=pk2[:].rearrange("p t o -> p o t"))
+            wgs.append(wg2)
             nc.vector.quantize_mx(
-                out=w_codes[:, 2, :].bitcast(FP8X4), scales=w_scales[:, 2, :], in_=wg2[:]
+                out=w_codes[:, g - 1, :].bitcast(FP8X4), scales=w_scales[:, g - 1, :], in_=wgs[g - 1][:]
+            )
+        nc.vector.quantize_mx(out=w_codes[:, 2, :].bitcast(FP8X4), scales=w_scales[:, 2, :], in_=wgs[2][:])
+        rstd = setup.tile([P, NJ], F32)
+        nc.vector.reciprocal(rstd[:], std[:])
+        nc.vector.tensor_mul(out=bn_scale[:], in0=vecs[:, 1], in1=rstd[:])
+        diff = setup.tile([P, NJ], F32)
+        nc.vector.tensor_sub(out=diff[:], in0=vecs[:, 0], in1=vecs[:, 3])
+        nc.vector.tensor_mul(out=diff[:], in0=diff[:], in1=bn_scale[:])
+        nc.vector.tensor_add(out=bn_shift[:], in0=diff[:], in1=vecs[:, 2])
+
+        T_BANKS = [(gi, r0, min(4, NR - r0)) for gi in range(2) for r0 in range(0, NR, 4)]
+
+        def turn_in(ch, banks, use_vector=False):
+            for gi, r0, nr in banks:
+                if (ch, gi + 1) not in grps:
+                    grp = grp_pool.tile([P, 4 * COLS], BF16, tag="grp", align_bytes=64)
+                    grps[(ch, gi + 1)] = grp
+                words = x2s[ch][:, gi].bitcast(F32).rearrange("p (c r) -> p r c", r=NR)
+                pin = psum_t.tile([P, 4, P], F32, tag="bank")
+                for k in range(nr):
+                    nc.tensor.transpose(pin[:, k, :], words[:, r0 + k, :], ident_f[:])
+                dst = grps[(ch, gi + 1)][:].rearrange(
+                    "p (b r e t) -> p r b e t", b=CB, r=NR, e=2, t=4
+                )[:, r0 : r0 + nr]
+                src = (
+                    pin[:, 0:nr, :]
+                    .rearrange("p r w -> p (r w)")
+                    .bitcast(BF16)
+                    .rearrange("p (r b t e) -> p r b e t", r=nr, b=CB, t=4)
+                )
+                if use_vector:
+                    nc.vector.tensor_copy(out=dst, in_=src)
+                else:
+                    nc.scalar.copy(out=dst, in_=src)
+
+        def group_up(ch, b0, b1):
+            if (ch, 0) not in grps:
+                grp = grp_pool.tile([P, 4 * COLS], BF16, tag="grp", align_bytes=64)
+                grps[(ch, 0)] = grp
+            nc.vector.tensor_copy(
+                out=grps[(ch, 0)][:].rearrange("p (b r e t) -> p b r t e", b=CB, r=NR, e=2)[:, b0:b1],
+                in_=raws[ch][:, b0:b1].rearrange("p b t (r e) -> p b r t e", e=2),
             )
 
-            ftT = setup.tile([P, NJ, P], BF16)
-            pt = psum.tile([P, NJ, P], BF16, tag="bank")
-            for kc in range(NJ):
-                nc.tensor.transpose(pt[:, kc, :], ft_sb[:, kc * P : (kc + 1) * P], ident_bf[:])
-            nc.vector.tensor_copy(out=ftT[:], in_=pt[:])
-            wfcT = setup.tile([P, NJ, C], BF16)
-            for kc in range(NJ):
-                pk = psum.tile([P, NJ, P], BF16, tag="bank")
-                for j in range(NJ):
-                    nc.tensor.transpose(pk[:, j, :], wfc_sb[:, j, kc * P : (kc + 1) * P], ident_bf[:])
-                nc.scalar.copy(out=wfcT[:, kc, :], in_=pk[:].rearrange("p j o -> p (j o)"))
-            pf = psum.tile([P, C], F32, tag="bank")
-            for kc in range(NJ):
-                nc.tensor.matmul(pf[:], lhsT=ftT[:, kc, :], rhs=wfcT[:, kc, :], start=(kc == 0), stop=False)
-            nc.tensor.matmul(pf[:], lhsT=ones_bf[:], rhs=bias_row[:], start=False, stop=True)
-            nc.vector.tensor_scalar_add(out=gate[:], in0=pf[:], scalar1=1.0)
-
-        with tc.tile_pool(name="ypool", bufs=1) as y_pool, tc.tile_pool(name="tmp", bufs=3) as tmp_pool, tc.manual_schedule():
-            y = y_pool.tile([P, NJ, PX, B], F32)
-
-            state = {}
-            grps = {}
-            SLICES = ((0, 8), (8, 16), (16, NR))
-
-            def turn_in(ch):
+        def quantise(ch, g):
+            if ch not in codes_of:
                 codes = code_pool.tile([P, NG, COLS], U32, align_bytes=64)
                 scales = code_pool.tile([P, NG, COLS], U8, align_bytes=64)
-                state[ch] = (codes, scales)
-                grp = grp_pool.tile([P, 4 * COLS], BF16, tag="grp", align_bytes=64)
-                grps[(ch, 2)] = grp
-                words = x2s[ch][:].bitcast(F32).rearrange("p (c r) -> p r c", r=NR)
-                for r0 in range(0, NR, 4):
-                    nr = min(4, NR - r0)
-                    pin = psum.tile([P, 4, P], F32, tag="bank")
-                    for k in range(nr):
-                        nc.tensor.transpose(pin[:, k, :], words[:, r0 + k, :], ident_f[:])
-                    nc.scalar.copy(
-                        out=grp[:, r0 * 4 * RCOLS : (r0 + nr) * 4 * RCOLS].rearrange(
-                            "p (q e t) -> p q e t", e=2, t=4
-                        ),
-                        in_=pin[:, 0:nr, :]
-                        .rearrange("p r w -> p (r w)")
-                        .bitcast(BF16)
-                        .rearrange("p (q t e) -> p q e t", t=4, e=2),
-                    )
-                if ch + 2 < NCH:
-                    load_x2(ch + 2)
-
-            def group_up(ch, g, parts):
-                if (ch, g) not in grps:
-                    grp = grp_pool.tile([P, 4 * COLS], BF16, tag="grp", align_bytes=64)
-                    grps[(ch, g)] = grp
-                for r0, r1 in parts:
-                    nc.vector.tensor_copy(
-                        out=grps[(ch, g)][:, r0 * 4 * RCOLS : r1 * 4 * RCOLS].rearrange(
-                            "p (r b e t) -> p b r t e", r=r1 - r0, b=CB, e=2, t=4
-                        ),
-                        in_=raws[ch][:, g, :, :, 2 * r0 : 2 * r1].rearrange("p b t (r e) -> p b r t e", e=2),
-                    )
-
-            def quantise(ch, g, parts):
-                codes, scales = state[ch]
-                for r0, r1 in parts:
-                    lo, hi = r0 * RCOLS, r1 * RCOLS
-                    nc.vector.quantize_mx(
-                        out=codes[:, g, lo:hi].bitcast(FP8X4),
-                        scales=scales[:, g, lo:hi],
-                        in_=grps[(ch, g)][:, 4 * lo : 4 * hi],
-                    )
-
-            def mx_pass(acc, j, g, ch, part):
-                codes, scales = state[ch]
-                lo, hi = part[0] * RCOLS, part[1] * RCOLS
-                nc.tensor.matmul_mx(
-                    out=acc[:, 0 : hi - lo],
-                    lhsT=w_codes[:, g, j * P : (j + 1) * P].bitcast(FP8X4),
-                    lhsT_scale=w_scales[:, g, j * P : (j + 1) * P],
-                    rhs=codes[:, g, lo:hi].bitcast(FP8X4),
-                    rhs_scale=scales[:, g, lo:hi],
-                    start=(g == G_ORDER[0]),
-                    stop=(g == G_ORDER[-1]),
+                codes_of[ch] = (codes, scales)
+            codes, scales = codes_of[ch]
+            for lo, hi in ((0, 1024), (1024, COLS)):
+                nc.vector.quantize_mx(
+                    out=codes[:, g, lo:hi].bitcast(FP8X4),
+                    scales=scales[:, g, lo:hi],
+                    in_=grps[(ch, g)][:, 4 * lo : 4 * hi],
                 )
 
-            def leave(acc, j, ch, part, use_vector):
-                r0, r1 = part
-                b0 = ch * CB
-                dst = y[:, j, 2 * r0 : 2 * r1, b0 : b0 + CB].rearrange("o (r e) b -> o r b e", e=2)
-                src = acc[:, 0 : (r1 - r0) * RCOLS].rearrange("o (r b e) -> o r b e", r=r1 - r0, b=CB, e=2)
-                if use_vector:
+        ys, osts = {}, {}
+
+        def multiply(ch, part, js, vector_js=()):
+            codes, scales = codes_of[ch]
+            lo, hi = SLICES[part]
+            if ch not in ys:
+                y = y_pool.tile([P, NJ, COLS], F32, tag="y")
+                ys[ch] = y
+            for j in js:
+                acc = psum_m.tile([P, 512], F32, tag="bank")
+                for g in range(NG):
+                    nc.tensor.matmul_mx(
+                        out=acc[:, 0 : hi - lo],
+                        lhsT=w_codes[:, g, j * P : (j + 1) * P].bitcast(FP8X4),
+                        lhsT_scale=w_scales[:, g, j * P : (j + 1) * P],
+                        rhs=codes[:, g, lo:hi].bitcast(FP8X4),
+                        rhs_scale=scales[:, g, lo:hi],
+                        start=(g == 0),
+                        stop=(g == NG - 1),
+                    )
+                if j in vector_js:
                     nc.vector.tensor_scalar(
-                        out=dst,
-                        in0=src,
+                        out=ys[ch][:, j, lo:hi],
+                        in0=acc[:, 0 : hi - lo],
                         scalar1=bn_scale[:, j : j + 1],
                         scalar2=bn_shift[:, j : j + 1],
                         op0=ALU.mult,
@@ -254,106 +211,96 @@ def tile_joint_module_pa_t_kernel(tc, fv, ft, W1, b1, g1, be1, m1, v1, Wfc1, bfc
                     )
                 else:
                     nc.scalar.activation(
-                        out=dst,
-                        in_=src,
+                        out=ys[ch][:, j, lo:hi],
+                        in_=acc[:, 0 : hi - lo],
                         func=ACT.Identity,
                         bias=bn_shift[:, j : j + 1],
                         scale=bn_scale[:, j : j + 1],
                     )
 
-            def whole_group(j, ch, part, use_vector):
-                acc = psum.tile([P, WIDE], F32, tag="bank")
-                for g in G_ORDER:
-                    mx_pass(acc, j, g, ch, part)
-                leave(acc, j, ch, part, use_vector)
-
-            ALL = ((0, 16), (16, NR))
-            open_acc = {}
-
-            def finish(j):
-                for part in SLICES[0:2]:
-                    mx_pass(open_acc[(j, part)], j, 1, LAST, part)
-                    leave(open_acc[(j, part)], j, LAST, part, False)
-                whole_group(j, LAST, SLICES[2], True)
-
-            turn_in(0)
-            for ch in range(NCH):
-                group_up(ch, 0, ((0, NR),))
-                quantise(ch, 2, ALL)
-                if ch + 1 < NCH:
-                    turn_in(ch + 1)
-                else:
-                    for j in J_ORDER:
-                        for part in SLICES[0:2]:
-                            acc = psum.tile([P, WIDE], F32, tag="bank")
-                            open_acc[(j, part)] = acc
-                            mx_pass(acc, j, 2, ch, part)
-                quantise(ch, 0, ALL)
-                if ch == LAST:
-                    for j in J_ORDER:
-                        for part in SLICES[0:2]:
-                            mx_pass(open_acc[(j, part)], j, 0, ch, part)
-                group_up(ch, 1, SLICES[0:2])
-                quantise(ch, 1, SLICES[0:1])
-                group_up(ch, 1, SLICES[2:3])
-                quantise(ch, 1, SLICES[1:3])
-                if ch + 2 < NCH:
-                    load_raw(ch + 2)
-                if ch < LAST:
-                    for part in SLICES:
-                        for j in range(NJ):
-                            whole_group(j, ch, part, False)
-            finish(J_ORDER[0])
-            finish(J_ORDER[1])
-
-            osts = {}
-
-            def turn(j, q):
-                if q == 0:
-                    ost = big_pool.tile([P, P, PX], F32, tag="big")
-                    osts[j] = ost
-                tr = psum.tile([P, 4, P], F32, tag="bank")
-                for x in range(4):
-                    nc.tensor.transpose(tr[:, x, :], y[:, j, 4 * q + x, :], ident_f[:])
-                return tr
-
-            def store(j):
-                nc.sync.dma_start(
-                    out=out[:, j * P : (j + 1) * P].rearrange("b o h w -> b (o h w)"),
-                    in_=osts[j][:].rearrange("b o x -> b (o x)"),
-                )
-
-            def gate_of(j):
-                return gate[:, j * P : (j + 1) * P].unsqueeze(2).to_broadcast([P, P, 4])
-
-            def on_vector(j, q):
-                tr = turn(j, q)
+        def finish(ch, part, js):
+            if ch not in osts:
+                ost = ost_pool.tile([P, CB, NJ, PX], F32, tag="ost")
+                osts[ch] = ost
+            s0, s1 = SAMPLES[part]
+            for j in js:
                 nc.vector.scalar_tensor_tensor(
-                    out=osts[j][:, :, 4 * q : 4 * q + 4],
-                    in0=tr[:].rearrange("b x o -> b o x"),
+                    out=osts[ch][:, s0:s1, j, :],
+                    in0=ys[ch][:, j, s0 * PX : s1 * PX].rearrange("p (b x) -> p b x", x=PX),
                     scalar=0.0,
-                    in1=gate_of(j),
+                    in1=gate[:, j, ch * CB + s0 : ch * CB + s1].unsqueeze(2).to_broadcast([P, s1 - s0, PX]),
                     op0=ALU.max,
                     op1=ALU.mult,
                 )
-                if q == NQ - 1:
-                    store(j)
 
-            def on_scalar_gpsimd(j, q):
-                tr = turn(j, q)
-                tmp = tmp_pool.tile([P, P, 4], F32, tag="tmp")
-                nc.scalar.activation(out=tmp[:], in_=tr[:].rearrange("b x o -> b o x"), func=ACT.Relu)
-                nc.gpsimd.tensor_tensor(
-                    out=osts[j][:, :, 4 * q : 4 * q + 4], in0=tmp[:], in1=gate_of(j), op=ALU.mult
+        def store(ch, s0, s1):
+            b0 = ch * CB
+            nc.sync.dma_start(
+                out=out[b0 + s0 : b0 + s1].rearrange("b (p j) h w -> p b (j h w)", j=NJ),
+                in_=osts[ch][:, s0:s1].rearrange("p b j x -> p b (j x)"),
+            )
+
+        half = len(T_BANKS) // 2
+        turn_in(0, T_BANKS[0:half])
+        group_up(0, 0, CB)
+        quantise(0, 1)
+        turn_in(0, T_BANKS[half:])
+        quantise(0, 0)
+        quantise(0, 2)
+
+        ftT = setup.tile([P, NJ, P], BF16)
+        pt = psum_m.tile([P, NJ, P], BF16, tag="bank")
+        for kc in range(NJ):
+            nc.tensor.transpose(pt[:, kc, :], ft_sb[:, kc * P : (kc + 1) * P], ident_bf[:])
+        nc.scalar.copy(out=ftT[:], in_=pt[:])
+        wfcT = setup.tile([P, NJ, NJ, P], BF16)
+        for kc in range(NJ):
+            pk = psum_m.tile([P, NJ, P], BF16, tag="bank")
+            for j in range(NJ):
+                nc.tensor.transpose(pk[:, j, :], wfc_sb[:, j, kc * P : (kc + 1) * P], ident_bf[:])
+            nc.scalar.copy(out=wfcT[:, kc], in_=pk[:])
+        pf = psum_m.tile([P, NJ, P], F32, tag="bank")
+        for j in range(NJ):
+            for kc in range(NJ):
+                nc.tensor.matmul(
+                    pf[:, j, :], lhsT=wfcT[:, kc, j, :], rhs=ftT[:, kc, :], start=(kc == 0), stop=(kc == NJ - 1)
                 )
-                if q == NQ - 1:
-                    store(j)
+        for j in range(NJ):
+            nc.vector.tensor_scalar(
+                out=gate[:, j, :],
+                in0=pf[:, j, :],
+                scalar1=vecs[:, 5, j : j + 1],
+                scalar2=1.0,
+                op0=ALU.add,
+                op1=ALU.add,
+            )
 
-            for i in range(3 * NQ):
-                on_vector(J_VECTOR[i // NQ], i % NQ)
-                if i % 2 == 1 and i < 2 * NQ:
-                    on_scalar_gpsimd(J_ORDER[1], i // 2)
-                if i == 1:
-                    finish(J_ORDER[2])
-                if i == 5:
-                    finish(J_ORDER[3])
+        third = -(-len(T_BANKS) // 3)
+        for ch in range(NCH):
+            nxt = ch + 1
+            more = nxt < NCH
+            if ch + 2 < NCH:
+                load_x2(ch + 2)
+                load_raw(ch + 2)
+            if more:
+                turn_in(nxt, T_BANKS[0:third])
+                group_up(nxt, 0, 16)
+            multiply(ch, 0, range(NJ), () if more else (1, 3))
+            if more:
+                group_up(nxt, 16, CB)
+                turn_in(nxt, T_BANKS[third : 2 * third])
+            finish(ch, 0, range(NJ))
+            multiply(ch, 1, (0, 1), () if more else (1,))
+            if more:
+                quantise(nxt, 0)
+                turn_in(nxt, T_BANKS[2 * third :])
+            multiply(ch, 1, (2, 3), () if more else (3,))
+            if more:
+                quantise(nxt, 1)
+            finish(ch, 1, range(NJ))
+            multiply(ch, 2, range(NJ), () if more else (1, 3))
+            store(ch, 0, 28)
+            if more:
+                quantise(nxt, 2)
+            finish(ch, 2, range(NJ))
+            store(ch, 28, CB)

@@ -18,6 +18,7 @@ EPS = 1e-5
 NG = 3
 NJ = 4
 CB = 32
+V_BANKS = (2, 4, 9)
 NCH = B // CB
 NR = PX // 2
 COLS = CB * PX
@@ -58,21 +59,22 @@ def tile_joint_module_pa_t_kernel(tc, fv, ft, W1, b1, g1, be1, m1, v1, Wfc1, bfc
         def load_x2(ch):
             b0 = ch * CB
             x2c = x2_pool.tile([P, 2, P * PX], BF16, tag="x2c")
-            for t in range(4):
-                nc.sync.dma_start(
-                    out=x2c[t : P : 4],
-                    in_=fv[b0 : b0 + CB, C:]
-                    .rearrange("b (g q c) h w -> b g q (c h w)", g=2, q=4)[:, :, t],
-                )
+            for gi in range(2):
+                for t in range(4):
+                    c0 = (gi + 1) * C + t * P
+                    nc.sync.dma_start(
+                        out=x2c[t : P : 4, gi], in_=fv[b0 : b0 + CB, c0 : c0 + P].rearrange("b c h w -> b (c h w)")
+                    )
             x2s[ch] = x2c
 
         def load_raw(ch):
             b0 = ch * CB
             raw = raw_pool.tile([P, CB, 4, PX], BF16, tag="raw")
-            nc.sync.dma_start(
-                out=raw[:].rearrange("p b t x -> p b (t x)"),
-                in_=fv[b0 : b0 + CB, 0:C].rearrange("b (p t) h w -> p b (t h w)", t=4),
-            )
+            for s0 in (0, CB // 2):
+                nc.sync.dma_start(
+                    out=raw[:, s0 : s0 + CB // 2].rearrange("p b t x -> p b (t x)"),
+                    in_=fv[b0 + s0 : b0 + s0 + CB // 2, 0:C].rearrange("b (p t) h w -> p b (t h w)", t=4),
+                )
             raws[ch] = raw
 
         vec_rows = setup.tile([P, C], BF16)
@@ -107,9 +109,11 @@ def tile_joint_module_pa_t_kernel(tc, fv, ft, W1, b1, g1, be1, m1, v1, Wfc1, bfc
             for jj in range(2):
                 for u in range(2):
                     nc.tensor.transpose(pw[:, jj, u, :], w_words[:, 2 * jp + jj, 0, u, :], ident_f[:])
-            nc.vector.tensor_copy(
-                out=wg_words[:, 2 * jp : 2 * jp + 2], in_=pw[:].rearrange("p j u o -> p j o u")
-            )
+            dst, src = wg_words[:, 2 * jp : 2 * jp + 2], pw[:].rearrange("p j u o -> p j o u")
+            if jp == 0:
+                nc.vector.tensor_copy(out=dst, in_=src)
+            else:
+                nc.scalar.copy(out=dst, in_=src)
         wgs = [wg]
         for g in (1, 2):
             wg2 = wg_pool.tile([P, 4 * C], BF16, tag="wg", align_bytes=64)
@@ -119,7 +123,11 @@ def tile_joint_module_pa_t_kernel(tc, fv, ft, W1, b1, g1, be1, m1, v1, Wfc1, bfc
                 for t in range(4):
                     c0 = j * C3 + g * C + t * P
                     nc.tensor.transpose(pk2[:, t, :], w1_sb[:, c0 : c0 + P], ident_bf[:])
-                nc.vector.tensor_copy(out=wg2_v[:, j], in_=pk2[:].rearrange("p t o -> p o t"))
+                dst, src = wg2_v[:, j], pk2[:].rearrange("p t o -> p o t")
+                if j % 2 == 0:
+                    nc.vector.tensor_copy(out=dst, in_=src)
+                else:
+                    nc.scalar.copy(out=dst, in_=src)
             wgs.append(wg2)
             nc.vector.quantize_mx(
                 out=w_codes[:, g - 1, :].bitcast(FP8X4), scales=w_scales[:, g - 1, :], in_=wgs[g - 1][:]
@@ -135,8 +143,9 @@ def tile_joint_module_pa_t_kernel(tc, fv, ft, W1, b1, g1, be1, m1, v1, Wfc1, bfc
 
         T_BANKS = [(gi, r0, min(4, NR - r0)) for gi in range(2) for r0 in range(0, NR, 4)]
 
-        def turn_in(ch, banks, use_vector=False):
-            for gi, r0, nr in banks:
+        def turn_in(ch, lo, hi, on_vector=V_BANKS):
+            for i in range(lo, hi):
+                gi, r0, nr = T_BANKS[i]
                 if (ch, gi + 1) not in grps:
                     grp = grp_pool.tile([P, 4 * COLS], BF16, tag="grp", align_bytes=64)
                     grps[(ch, gi + 1)] = grp
@@ -153,7 +162,7 @@ def tile_joint_module_pa_t_kernel(tc, fv, ft, W1, b1, g1, be1, m1, v1, Wfc1, bfc
                     .bitcast(BF16)
                     .rearrange("p (r b t e) -> p r b e t", r=nr, b=CB, t=4)
                 )
-                if use_vector:
+                if i in on_vector:
                     nc.vector.tensor_copy(out=dst, in_=src)
                 else:
                     nc.scalar.copy(out=dst, in_=src)
@@ -163,17 +172,17 @@ def tile_joint_module_pa_t_kernel(tc, fv, ft, W1, b1, g1, be1, m1, v1, Wfc1, bfc
                 grp = grp_pool.tile([P, 4 * COLS], BF16, tag="grp", align_bytes=64)
                 grps[(ch, 0)] = grp
             nc.vector.tensor_copy(
-                out=grps[(ch, 0)][:].rearrange("p (b r e t) -> p b r t e", b=CB, r=NR, e=2)[:, b0:b1],
-                in_=raws[ch][:, b0:b1].rearrange("p b t (r e) -> p b r t e", e=2),
+                out=grps[(ch, 0)][:].rearrange("p (b q i t) -> p b q t i", b=CB, i=4, t=4)[:, b0:b1],
+                in_=raws[ch][:, b0:b1].rearrange("p b t (q i) -> p b q t i", i=4),
             )
 
-        def quantise(ch, g):
+        def quantise(ch, g, cuts=((0, 1024), (1024, COLS))):
             if ch not in codes_of:
                 codes = code_pool.tile([P, NG, COLS], U32, align_bytes=64)
                 scales = code_pool.tile([P, NG, COLS], U8, align_bytes=64)
                 codes_of[ch] = (codes, scales)
             codes, scales = codes_of[ch]
-            for lo, hi in ((0, 1024), (1024, COLS)):
+            for lo, hi in cuts:
                 nc.vector.quantize_mx(
                     out=codes[:, g, lo:hi].bitcast(FP8X4),
                     scales=scales[:, g, lo:hi],
@@ -240,42 +249,45 @@ def tile_joint_module_pa_t_kernel(tc, fv, ft, W1, b1, g1, be1, m1, v1, Wfc1, bfc
                 in_=osts[ch][:, s0:s1].rearrange("p b j x -> p b (j x)"),
             )
 
-        half = len(T_BANKS) // 2
-        turn_in(0, T_BANKS[0:half])
-        group_up(0, 0, CB)
-        quantise(0, 1)
-        turn_in(0, T_BANKS[half:])
-        quantise(0, 0)
-        quantise(0, 2)
-
         ftT = setup.tile([P, NJ, P], BF16)
-        pt = psum_m.tile([P, NJ, P], BF16, tag="bank")
-        for kc in range(NJ):
-            nc.tensor.transpose(pt[:, kc, :], ft_sb[:, kc * P : (kc + 1) * P], ident_bf[:])
-        nc.scalar.copy(out=ftT[:], in_=pt[:])
         wfcT = setup.tile([P, NJ, NJ, P], BF16)
-        for kc in range(NJ):
-            pk = psum_m.tile([P, NJ, P], BF16, tag="bank")
-            for j in range(NJ):
-                nc.tensor.transpose(pk[:, j, :], wfc_sb[:, j, kc * P : (kc + 1) * P], ident_bf[:])
-            nc.scalar.copy(out=wfcT[:, kc], in_=pk[:])
-        pf = psum_m.tile([P, NJ, P], F32, tag="bank")
-        for j in range(NJ):
-            for kc in range(NJ):
-                nc.tensor.matmul(
-                    pf[:, j, :], lhsT=wfcT[:, kc, j, :], rhs=ftT[:, kc, :], start=(kc == 0), stop=(kc == NJ - 1)
-                )
-        for j in range(NJ):
-            nc.vector.tensor_scalar(
-                out=gate[:, j, :],
-                in0=pf[:, j, :],
-                scalar1=vecs[:, 5, j : j + 1],
-                scalar2=1.0,
-                op0=ALU.add,
-                op1=ALU.add,
-            )
 
-        third = -(-len(T_BANKS) // 3)
+        def make_gate():
+            pt = psum_t.tile([P, NJ, P], BF16, tag="bank")
+            for kc in range(NJ):
+                nc.tensor.transpose(pt[:, kc, :], ft_sb[:, kc * P : (kc + 1) * P], ident_bf[:])
+            nc.scalar.copy(out=ftT[:], in_=pt[:])
+            for kc in range(NJ):
+                pk = psum_t.tile([P, NJ, P], BF16, tag="bank")
+                for j in range(NJ):
+                    nc.tensor.transpose(pk[:, j, :], wfc_sb[:, j, kc * P : (kc + 1) * P], ident_bf[:])
+                nc.scalar.copy(out=wfcT[:, kc], in_=pk[:])
+            pf = psum_t.tile([P, NJ, P], F32, tag="bank")
+            for j in range(NJ):
+                for kc in range(NJ):
+                    nc.tensor.matmul(
+                        pf[:, j, :], lhsT=wfcT[:, kc, j, :], rhs=ftT[:, kc, :], start=(kc == 0), stop=(kc == NJ - 1)
+                    )
+            for j in range(NJ):
+                nc.vector.tensor_scalar(
+                    out=gate[:, j, :],
+                    in0=pf[:, j, :],
+                    scalar1=vecs[:, 5, j : j + 1],
+                    scalar2=1.0,
+                    op0=ALU.add,
+                    op1=ALU.add,
+                )
+
+
+        turn_in(0, 0, 5, (1, 3))
+        group_up(0, 0, 16)
+        turn_in(0, 5, 10, (6, 8))
+        quantise(0, 1)
+        quantise(0, 0, ((0, 512),))
+        quantise(0, 2)
+        group_up(0, 16, CB)
+        quantise(0, 0, ((512, 1024), (1024, COLS)))
+
         for ch in range(NCH):
             nxt = ch + 1
             more = nxt < NCH
@@ -283,23 +295,31 @@ def tile_joint_module_pa_t_kernel(tc, fv, ft, W1, b1, g1, be1, m1, v1, Wfc1, bfc
                 load_x2(ch + 2)
                 load_raw(ch + 2)
             if more:
-                turn_in(nxt, T_BANKS[0:third])
+                turn_in(nxt, 0, 2)
                 group_up(nxt, 0, 16)
-            multiply(ch, 0, range(NJ), () if more else (1, 3))
+            multiply(ch, 0, (0, 1), () if more else (1,))
             if more:
+                turn_in(nxt, 2, 4)
                 group_up(nxt, 16, CB)
-                turn_in(nxt, T_BANKS[third : 2 * third])
+            multiply(ch, 0, (2, 3), () if more else (3,))
+            if ch == 0:
+                make_gate()
+            if more:
+                turn_in(nxt, 4, 6)
+                quantise(nxt, 0)
             finish(ch, 0, range(NJ))
+            if not more:
+                store(ch, 0, 14)
             multiply(ch, 1, (0, 1), () if more else (1,))
             if more:
-                quantise(nxt, 0)
-                turn_in(nxt, T_BANKS[2 * third :])
+                turn_in(nxt, 6, 8)
+                quantise(nxt, 1)
             multiply(ch, 1, (2, 3), () if more else (3,))
             if more:
-                quantise(nxt, 1)
+                turn_in(nxt, 8, 10)
             finish(ch, 1, range(NJ))
             multiply(ch, 2, range(NJ), () if more else (1, 3))
-            store(ch, 0, 28)
+            store(ch, 0 if more else 14, 28)
             if more:
                 quantise(nxt, 2)
             finish(ch, 2, range(NJ))

@@ -18,12 +18,20 @@ EPS = 1e-5
 NG = 3
 NJ = 4
 CB = 32
-V_BANKS = (2, 4, 9)
 NCH = B // CB
+LAST = NCH - 1
+HB = CB // 2
+NU = B // HB
 NR = PX // 2
 COLS = CB * PX
-SLICES = ((0, 512), (512, 1024), (1024, COLS))
-SAMPLES = ((0, 14), (14, 28), (28, CB))
+CUTS = (((0, 512),), ((512, 1024), (1024, COLS)))
+SAMPLES = ((0, 14), (14, CB))
+Y_SHIFT = 8
+G_ORDER = (0, 1, 2)
+TURNED = ((1, 2), (1, 2), (1, 2), (1, 2))
+LEAD = 4
+V_SHARE = {0: (0, 2, 4, 6, 8)}
+S_SAMPLES = {5: 4, 6: 4}
 
 FLOPS = 2 * C * C3 * B * PX + 2 * B * C * C
 
@@ -32,225 +40,279 @@ def tile_joint_module_pa_t_kernel(tc, fv, ft, W1, b1, g1, be1, m1, v1, Wfc1, bfc
     nc = tc.nc
     with ExitStack() as ctx:
         keep = ctx.enter_context(tc.tile_pool(name="keep", bufs=1))
-        psum_t = ctx.enter_context(tc.psum_pool(name="psum_t", bufs=4))
-        psum_m = ctx.enter_context(tc.psum_pool(name="psum_m", bufs=4))
-        x2_pool = ctx.enter_context(tc.tile_pool(name="x2", bufs=2))
-        raw_pool = ctx.enter_context(tc.tile_pool(name="raw", bufs=2))
-        grp_pool = ctx.enter_context(tc.tile_pool(name="grp", bufs=4))
+        psum_t = ctx.enter_context(tc.psum_pool(name="psum_t", bufs=3))
+        psum_m = ctx.enter_context(tc.psum_pool(name="psum_m", bufs=5))
+        x2_pool = ctx.enter_context(tc.tile_pool(name="x2", bufs=4))
+        raw_pool = ctx.enter_context(tc.tile_pool(name="raw", bufs=5))
+        grp_pool = ctx.enter_context(tc.tile_pool(name="grp", bufs=6))
         code_pool = ctx.enter_context(tc.tile_pool(name="code", bufs=2))
-        y_pool = ctx.enter_context(tc.tile_pool(name="y", bufs=1))
         ost_pool = ctx.enter_context(tc.tile_pool(name="ost", bufs=2))
-        setup = ctx.enter_context(tc.tile_pool(name="setup", bufs=1))
-        wg_pool = ctx.enter_context(tc.tile_pool(name="wg", bufs=2))
         ctx.enter_context(tc.manual_schedule())
 
         ident_bf = keep.tile([P, P], BF16)
         make_identity(nc, ident_bf[:])
         ident_f = keep.tile([P, P], F32)
         make_identity(nc, ident_f[:])
-        w_codes = keep.tile([P, NG, C], U32, align_bytes=64)
-        w_scales = keep.tile([P, NG, C], U8, align_bytes=64)
         gate = keep.tile([P, NJ, B], F32)
         bn_scale = keep.tile([P, NJ], F32)
         bn_shift = keep.tile([P, NJ], F32)
+        y = keep.tile([P, NJ, COLS + Y_SHIFT * LAST], F32)
+        warm = keep.tile([P, 1], F32)
+        nc.vector.memset(warm[:], 1.0)
+        nc.scalar.sqrt(warm[:], warm[:])
+        vec_rows = keep.tile([P, C], BF16)
+        nc.vector.memset(vec_rows[:], 0.0)
 
-        x2s, raws, grps, codes_of = {}, {}, {}, {}
+        x2s, raws, grps, codes_of, osts = {}, {}, {}, {}, {}
+
+        def load_turned(ch, g):
+            x2c = x2_pool.tile([P, P * PX], BF16, tag="x2c")
+            for t in range(4):
+                c0 = g * C + t * P
+                nc.sync.dma_start(
+                    out=x2c[t : P : 4, :],
+                    in_=fv[ch * CB : (ch + 1) * CB, c0 : c0 + P].rearrange("b c h w -> b (c h w)"),
+                )
+            x2s[(ch, g)] = x2c
 
         def load_x2(ch):
-            b0 = ch * CB
-            x2c = x2_pool.tile([P, 2, P * PX], BF16, tag="x2c")
-            for gi in range(2):
-                for t in range(4):
-                    c0 = (gi + 1) * C + t * P
+            for g in TURNED[ch]:
+                load_turned(ch, g)
+
+        def load_raw(u):
+            for g in range(NG):
+                if g not in TURNED[u // 2]:
+                    raw = raw_pool.tile([P, HB, 4 * PX], BF16, tag="raw")
                     nc.sync.dma_start(
-                        out=x2c[t : P : 4, gi], in_=fv[b0 : b0 + CB, c0 : c0 + P].rearrange("b c h w -> b (c h w)")
+                        out=raw[:],
+                        in_=fv[u * HB : (u + 1) * HB, g * C : (g + 1) * C].rearrange("b (p t) h w -> p b (t h w)", t=4),
                     )
-            x2s[ch] = x2c
+                    raws[(u, g)] = raw
 
-        def load_raw(ch):
-            b0 = ch * CB
-            raw = raw_pool.tile([P, CB, 4, PX], BF16, tag="raw")
-            for s0 in (0, CB // 2):
-                nc.sync.dma_start(
-                    out=raw[:, s0 : s0 + CB // 2].rearrange("p b t x -> p b (t x)"),
-                    in_=fv[b0 + s0 : b0 + s0 + CB // 2, 0:C].rearrange("b (p t) h w -> p b (t h w)", t=4),
-                )
-            raws[ch] = raw
-
-        vec_rows = setup.tile([P, C], BF16)
-        nc.vector.memset(vec_rows[:], 0.0)
-        w1_sb = setup.tile([P, NJ * C3], BF16)
+        w1_sb = ost_pool.tile([P, NJ * C3], BF16, tag="ost")
         nc.sync.dma_start(out=w1_sb[:], in_=W1.rearrange("(o j) c -> o (j c)", j=NJ))
         for i, vec in enumerate((b1, g1, be1, m1, v1, bfc1)):
             nc.scalar.dma_start(out=vec_rows[i : i + 1, :], in_=vec.rearrange("(o c) -> o c", o=1))
+        ft_sb = keep.tile([P, C], BF16)
+        wfc_sb = keep.tile([P, NJ, C], BF16)
         load_x2(0)
         load_raw(0)
-        ft_sb = setup.tile([P, C], BF16)
-        nc.sync.dma_start(out=ft_sb[:], in_=ft)
-        wfc_sb = setup.tile([P, NJ, C], BF16)
-        nc.sync.dma_start(out=wfc_sb[:], in_=Wfc1.rearrange("(o j) k -> o j k", j=NJ))
-        load_x2(1)
         load_raw(1)
-
-        pv = psum_t.tile([P, NJ, P], BF16, tag="bank")
-        for j in range(NJ):
-            nc.tensor.transpose(pv[:, j, :], vec_rows[:, j : C : NJ], ident_bf[:])
-        vecs = setup.tile([P, 6, NJ], F32)
-        nc.vector.tensor_copy(out=vecs[:].rearrange("p i j -> p j i"), in_=pv[:, :, 0:6])
-        std = setup.tile([P, NJ], F32)
-        nc.vector.tensor_scalar_add(out=std[:], in0=vecs[:, 4], scalar1=EPS)
-        nc.scalar.sqrt(std[:], std[:])
+        load_x2(1)
+        load_raw(2)
+        nc.sync.dma_start(out=ft_sb[:], in_=ft)
+        nc.sync.dma_start(out=wfc_sb[:], in_=Wfc1.rearrange("(o j) k -> o j k", j=NJ))
+        load_raw(3)
 
         w_words = w1_sb[:].bitcast(F32).rearrange("o (j g p u) -> o j g u p", j=NJ, g=NG, p=P, u=2)
-        wg = wg_pool.tile([P, 4 * C], BF16, tag="wg", align_bytes=64)
-        wg_words = wg[:].bitcast(F32).rearrange("p (j o u) -> p j o u", j=NJ, o=P, u=2)
-        for jp in range(NJ // 2):
-            pw = psum_m.tile([P, 2, 2, P], F32, tag="bank")
-            for jj in range(2):
-                for u in range(2):
-                    nc.tensor.transpose(pw[:, jj, u, :], w_words[:, 2 * jp + jj, 0, u, :], ident_f[:])
-            dst, src = wg_words[:, 2 * jp : 2 * jp + 2], pw[:].rearrange("p j u o -> p j o u")
-            if jp == 0:
+        w_of = {}
+
+        def copy(on_vector, dst, src):
+            if on_vector:
                 nc.vector.tensor_copy(out=dst, in_=src)
             else:
                 nc.scalar.copy(out=dst, in_=src)
-        wgs = [wg]
-        for g in (1, 2):
-            wg2 = wg_pool.tile([P, 4 * C], BF16, tag="wg", align_bytes=64)
-            wg2_v = wg2[:].rearrange("p (j o t) -> p j o t", j=NJ, o=P, t=4)
-            for j in range(NJ):
-                pk2 = psum_m.tile([P, 4, P], BF16, tag="bank")
-                for t in range(4):
-                    c0 = j * C3 + g * C + t * P
-                    nc.tensor.transpose(pk2[:, t, :], w1_sb[:, c0 : c0 + P], ident_bf[:])
-                dst, src = wg2_v[:, j], pk2[:].rearrange("p t o -> p o t")
-                if j % 2 == 0:
-                    nc.vector.tensor_copy(out=dst, in_=src)
-                else:
-                    nc.scalar.copy(out=dst, in_=src)
-            wgs.append(wg2)
-            nc.vector.quantize_mx(
-                out=w_codes[:, g - 1, :].bitcast(FP8X4), scales=w_scales[:, g - 1, :], in_=wgs[g - 1][:]
-            )
-        nc.vector.quantize_mx(out=w_codes[:, 2, :].bitcast(FP8X4), scales=w_scales[:, 2, :], in_=wgs[2][:])
-        rstd = setup.tile([P, NJ], F32)
-        nc.vector.reciprocal(rstd[:], std[:])
-        nc.vector.tensor_mul(out=bn_scale[:], in0=vecs[:, 1], in1=rstd[:])
-        diff = setup.tile([P, NJ], F32)
-        nc.vector.tensor_sub(out=diff[:], in0=vecs[:, 0], in1=vecs[:, 3])
-        nc.vector.tensor_mul(out=diff[:], in0=diff[:], in1=bn_scale[:])
-        nc.vector.tensor_add(out=bn_shift[:], in0=diff[:], in1=vecs[:, 2])
 
-        T_BANKS = [(gi, r0, min(4, NR - r0)) for gi in range(2) for r0 in range(0, NR, 4)]
+        def turn_w(g, turned):
+            wg = grp_pool.tile([P, 4 * C], BF16, tag="grp", align_bytes=64)
+            if turned:
+                for j in range(NJ):
+                    pk = psum_m.tile([P, 4, P], BF16, tag="bank")
+                    for t in range(4):
+                        c0 = j * C3 + g * C + t * P
+                        nc.tensor.transpose(pk[:, t, :], w1_sb[:, c0 : c0 + P], ident_bf[:])
+                    dst = wg[:].rearrange("p (j o t) -> p j o t", j=NJ, o=P, t=4)[:, j]
+                    copy(j % 2 == 0, dst, pk[:].rearrange("p t o -> p o t"))
+            else:
+                for jp in range(NJ // 2):
+                    pw = psum_m.tile([P, 2, 2, P], F32, tag="bank")
+                    for jj in range(2):
+                        for w in range(2):
+                            nc.tensor.transpose(pw[:, jj, w, :], w_words[:, 2 * jp + jj, g, w, :], ident_f[:])
+                    dst = wg[:].bitcast(F32).rearrange("p (j o w) -> p j o w", j=NJ, o=P, w=2)
+                    copy(jp == 0, dst[:, 2 * jp : 2 * jp + 2], pw[:].rearrange("p j w o -> p j o w"))
+            return wg
 
-        def turn_in(ch, lo, hi, on_vector=V_BANKS):
-            for i in range(lo, hi):
-                gi, r0, nr = T_BANKS[i]
-                if (ch, gi + 1) not in grps:
-                    grp = grp_pool.tile([P, 4 * COLS], BF16, tag="grp", align_bytes=64)
-                    grps[(ch, gi + 1)] = grp
-                words = x2s[ch][:, gi].bitcast(F32).rearrange("p (c r) -> p r c", r=NR)
-                pin = psum_t.tile([P, 4, P], F32, tag="bank")
-                for k in range(nr):
-                    nc.tensor.transpose(pin[:, k, :], words[:, r0 + k, :], ident_f[:])
-                dst = grps[(ch, gi + 1)][:].rearrange(
-                    "p (b r e t) -> p r b e t", b=CB, r=NR, e=2, t=4
-                )[:, r0 : r0 + nr]
-                src = (
-                    pin[:, 0:nr, :]
-                    .rearrange("p r w -> p (r w)")
-                    .bitcast(BF16)
-                    .rearrange("p (r b t e) -> p r b e t", r=nr, b=CB, t=4)
-                )
-                if i in on_vector:
-                    nc.vector.tensor_copy(out=dst, in_=src)
-                else:
-                    nc.scalar.copy(out=dst, in_=src)
+        def quantise_w(key, wg):
+            codes = keep.tile([P, C], U32, align_bytes=64, name="w_codes_%d_%d" % (key[0], int(key[1])))
+            scales = keep.tile([P, C], U8, align_bytes=64, name="w_scales_%d_%d" % (key[0], int(key[1])))
+            nc.vector.quantize_mx(out=codes[:].bitcast(FP8X4), scales=scales[:], in_=wg[:])
+            w_of[key] = (codes, scales)
 
-        def group_up(ch, b0, b1):
-            if (ch, 0) not in grps:
+        need = [(g, turned) for turned in (True, False) for g in range(NG) if any((g in TURNED[ch]) == turned for ch in range(NCH))]
+        early = [k for k in need if (k[0] in TURNED[0]) == k[1]]
+        late = [k for k in need if k not in early]
+        wgs = [(k, turn_w(*k)) for k in early]
+        for k, wg in wgs:
+            quantise_w(k, wg)
+
+        def group_tile(ch, g):
+            if (ch, g) not in grps:
                 grp = grp_pool.tile([P, 4 * COLS], BF16, tag="grp", align_bytes=64)
-                grps[(ch, 0)] = grp
-            nc.vector.tensor_copy(
-                out=grps[(ch, 0)][:].rearrange("p (b q i t) -> p b q t i", b=CB, i=4, t=4)[:, b0:b1],
-                in_=raws[ch][:, b0:b1].rearrange("p b t (q i) -> p b q t i", i=4),
+                grps[(ch, g)] = grp
+            return grps[(ch, g)]
+
+        def banks_of(ch):
+            return [(ch, g, r0) for g in TURNED[ch] for r0 in range(0, NR, 4)]
+
+        def turn_in(ch, g, r0, on_vector):
+            nr = min(4, NR - r0)
+            words = x2s[(ch, g)][:].bitcast(F32).rearrange("p (c r) -> p r c", r=NR)
+            pin = psum_t.tile([P, 4, P], F32, tag="bank")
+            for k in range(nr):
+                nc.tensor.transpose(pin[:, k, :], words[:, r0 + k, :], ident_f[:])
+            dst = group_tile(ch, g)[:].rearrange("p (b r e t) -> p r b e t", b=CB, r=NR, e=2, t=4)[:, r0 : r0 + nr]
+            src = (
+                pin[:, 0:nr, :]
+                .rearrange("p r w -> p (r w)")
+                .bitcast(BF16)
+                .rearrange("p (r b t e) -> p r b e t", r=nr, b=CB, t=4)
+            )
+            copy(on_vector, dst, src)
+
+        def unit_of(u, g):
+            return group_tile(u // 2, g)[:].rearrange("p (b x t) -> p b x t", b=CB, t=4)[
+                :, (u % 2) * HB : (u % 2 + 1) * HB
+            ]
+
+        def others_of(u):
+            return [g for g in range(NG) if g not in TURNED[u // 2]]
+
+        def regroup(u):
+            for g in others_of(u)[0:1]:
+                nc.vector.tensor_copy(
+                    out=unit_of(u, g).rearrange("p b (q i) t -> p b q t i", i=4),
+                    in_=raws[(u, g)][:].rearrange("p b (t q i) -> p b q t i", t=4, i=4),
+                )
+
+        X_CUTS = ((0, 16), (16, 32), (32, PX))
+
+        def pass_through(u, g, x0, x1):
+            src = raws[(u, g)][:].rearrange("p b (t x) -> p b x t", t=4)
+            n = 8 * (x1 - x0) * 4
+            pin = psum_t.tile([P, 2, 512], BF16, tag="bank")
+            for k in range(2):
+                nc.tensor.matmul(
+                    pin[:, k, 0:n], lhsT=ident_bf[:], rhs=src[:, 8 * k : 8 * k + 8, x0:x1], start=True, stop=True
+                )
+            nc.scalar.copy(
+                out=unit_of(u, g)[:, :, x0:x1].rearrange("p (k b) x t -> p k b (x t)", k=2),
+                in_=pin[:, :, 0:n].rearrange("p k (b n) -> p k b n", b=8),
             )
 
-        def quantise(ch, g, cuts=((0, 1024), (1024, COLS))):
+        def prepare(u):
+            ch = u // 2
             if ch not in codes_of:
                 codes = code_pool.tile([P, NG, COLS], U32, align_bytes=64)
                 scales = code_pool.tile([P, NG, COLS], U8, align_bytes=64)
                 codes_of[ch] = (codes, scales)
             codes, scales = codes_of[ch]
-            for lo, hi in cuts:
-                nc.vector.quantize_mx(
-                    out=codes[:, g, lo:hi].bitcast(FP8X4),
-                    scales=scales[:, g, lo:hi],
-                    in_=grps[(ch, g)][:, 4 * lo : 4 * hi],
+            for g in G_ORDER:
+                for lo, hi in CUTS[u % 2]:
+                    nc.vector.quantize_mx(
+                        out=codes[:, g, lo:hi].bitcast(FP8X4),
+                        scales=scales[:, g, lo:hi],
+                        in_=grps[(ch, g)][:, 4 * lo : 4 * hi],
+                    )
+
+        def multiply(u, lo, hi, j, on_vector):
+            ch = u // 2
+            codes, scales = codes_of[ch]
+            acc = psum_m.tile([P, 512], F32, tag="bank")
+            for g in G_ORDER:
+                wc, ws = w_of[(g, g in TURNED[ch])]
+                nc.tensor.matmul_mx(
+                    out=acc[:, 0 : hi - lo],
+                    lhsT=wc[:, j * P : (j + 1) * P].bitcast(FP8X4),
+                    lhsT_scale=ws[:, j * P : (j + 1) * P],
+                    rhs=codes[:, g, lo:hi].bitcast(FP8X4),
+                    rhs_scale=scales[:, g, lo:hi],
+                    start=(g == G_ORDER[0]),
+                    stop=(g == G_ORDER[-1]),
+                )
+            y0 = Y_SHIFT * (LAST - ch)
+            dst = y[:, j, y0 + lo : y0 + hi]
+            if on_vector:
+                nc.vector.tensor_scalar(
+                    out=dst,
+                    in0=acc[:, 0 : hi - lo],
+                    scalar1=bn_scale[:, j : j + 1],
+                    scalar2=bn_shift[:, j : j + 1],
+                    op0=ALU.mult,
+                    op1=ALU.add,
+                )
+            else:
+                nc.scalar.activation(
+                    out=dst,
+                    in_=acc[:, 0 : hi - lo],
+                    func=ACT.Relu,
+                    bias=bn_shift[:, j : j + 1],
+                    scale=bn_scale[:, j : j + 1],
                 )
 
-        ys, osts = {}, {}
-
-        def multiply(ch, part, js, vector_js=()):
-            codes, scales = codes_of[ch]
-            lo, hi = SLICES[part]
-            if ch not in ys:
-                y = y_pool.tile([P, NJ, COLS], F32, tag="y")
-                ys[ch] = y
-            for j in js:
-                acc = psum_m.tile([P, 512], F32, tag="bank")
-                for g in range(NG):
-                    nc.tensor.matmul_mx(
-                        out=acc[:, 0 : hi - lo],
-                        lhsT=w_codes[:, g, j * P : (j + 1) * P].bitcast(FP8X4),
-                        lhsT_scale=w_scales[:, g, j * P : (j + 1) * P],
-                        rhs=codes[:, g, lo:hi].bitcast(FP8X4),
-                        rhs_scale=scales[:, g, lo:hi],
-                        start=(g == 0),
-                        stop=(g == NG - 1),
-                    )
-                if j in vector_js:
-                    nc.vector.tensor_scalar(
-                        out=ys[ch][:, j, lo:hi],
-                        in0=acc[:, 0 : hi - lo],
-                        scalar1=bn_scale[:, j : j + 1],
-                        scalar2=bn_shift[:, j : j + 1],
-                        op0=ALU.mult,
-                        op1=ALU.add,
-                    )
-                else:
-                    nc.scalar.activation(
-                        out=ys[ch][:, j, lo:hi],
-                        in_=acc[:, 0 : hi - lo],
-                        func=ACT.Identity,
-                        bias=bn_shift[:, j : j + 1],
-                        scale=bn_scale[:, j : j + 1],
-                    )
-
-        def finish(ch, part, js):
+        def finish(u, s0, s1, on_scalar, with_relu):
+            ch = u // 2
             if ch not in osts:
                 ost = ost_pool.tile([P, CB, NJ, PX], F32, tag="ost")
                 osts[ch] = ost
-            s0, s1 = SAMPLES[part]
-            for j in js:
-                nc.vector.scalar_tensor_tensor(
-                    out=osts[ch][:, s0:s1, j, :],
-                    in0=ys[ch][:, j, s0 * PX : s1 * PX].rearrange("p (b x) -> p b x", x=PX),
-                    scalar=0.0,
-                    in1=gate[:, j, ch * CB + s0 : ch * CB + s1].unsqueeze(2).to_broadcast([P, s1 - s0, PX]),
-                    op0=ALU.max,
-                    op1=ALU.mult,
+            ost = osts[ch]
+            y0 = Y_SHIFT * (LAST - ch)
+            for b in range(s1 - on_scalar, s1):
+                for j in range(NJ):
+                    nc.scalar.activation(
+                        out=ost[:, b, j, :],
+                        in_=y[:, j, y0 + b * PX : y0 + (b + 1) * PX],
+                        func=ACT.Copy,
+                        scale=gate[:, j, ch * CB + b : ch * CB + b + 1],
+                    )
+            s1 -= on_scalar
+            yv = y[:, :, y0 + s0 * PX : y0 + s1 * PX].rearrange("p j (b x) -> p j b x", x=PX)
+            gv = gate[:, :, ch * CB + s0 : ch * CB + s1].unsqueeze(3)
+            if with_relu:
+                for j in range(NJ):
+                    nc.vector.scalar_tensor_tensor(
+                        out=ost[:, s0:s1, j, :],
+                        in0=yv[:, j],
+                        scalar=0.0,
+                        in1=gv[:, j].to_broadcast([P, s1 - s0, PX]),
+                        op0=ALU.max,
+                        op1=ALU.mult,
+                    )
+            else:
+                nc.vector.tensor_tensor(
+                    out=ost[:, s0:s1].rearrange("p b j x -> p j b x"),
+                    in0=yv,
+                    in1=gv.to_broadcast([P, NJ, s1 - s0, PX]),
+                    op=ALU.mult,
                 )
 
-        def store(ch, s0, s1):
-            b0 = ch * CB
+        def store(u, s0, s1):
+            b0 = (u // 2) * CB
             nc.sync.dma_start(
                 out=out[b0 + s0 : b0 + s1].rearrange("b (p j) h w -> p b (j h w)", j=NJ),
-                in_=osts[ch][:, s0:s1].rearrange("p b j x -> p b (j x)"),
+                in_=osts[u // 2][:, s0:s1].rearrange("p b j x -> p b (j x)"),
             )
 
-        ftT = setup.tile([P, NJ, P], BF16)
-        wfcT = setup.tile([P, NJ, NJ, P], BF16)
+        vecs = keep.tile([P, 6, NJ], F32)
+        std = keep.tile([P, NJ], F32)
+        rstd = keep.tile([P, NJ], F32)
+        diff = keep.tile([P, NJ], F32)
+
+        def make_batch_norm():
+            pv = psum_t.tile([P, NJ, P], BF16, tag="bank")
+            for j in range(NJ):
+                nc.tensor.transpose(pv[:, j, :], vec_rows[:, j : C : NJ], ident_bf[:])
+            nc.vector.tensor_copy(out=vecs[:].rearrange("p i j -> p j i"), in_=pv[:, :, 0:6])
+            nc.vector.tensor_scalar_add(out=std[:], in0=vecs[:, 4], scalar1=EPS)
+            nc.scalar.sqrt(std[:], std[:])
+            nc.vector.reciprocal(rstd[:], std[:])
+            nc.vector.tensor_mul(out=bn_scale[:], in0=vecs[:, 1], in1=rstd[:])
+            nc.vector.tensor_sub(out=diff[:], in0=vecs[:, 0], in1=vecs[:, 3])
+            nc.vector.tensor_mul(out=diff[:], in0=diff[:], in1=bn_scale[:])
+            nc.vector.tensor_add(out=bn_shift[:], in0=diff[:], in1=vecs[:, 2])
+
+        ftT = keep.tile([P, NJ, P], BF16)
+        wfcT = keep.tile([P, NJ, NJ, P], BF16)
 
         def make_gate():
             pt = psum_t.tile([P, NJ, P], BF16, tag="bank")
@@ -278,49 +340,51 @@ def tile_joint_module_pa_t_kernel(tc, fv, ft, W1, b1, g1, be1, m1, v1, Wfc1, bfc
                     op1=ALU.add,
                 )
 
+        for i, bank in enumerate(banks_of(0)):
+            turn_in(*bank, i in (1, 3, 5, 7))
+        regroup(0)
+        make_batch_norm()
+        prepare(0)
+        load_x2(2)
+        regroup(1)
 
-        turn_in(0, 0, 5, (1, 3))
-        group_up(0, 0, 16)
-        turn_in(0, 5, 10, (6, 8))
-        quantise(0, 1)
-        quantise(0, 0, ((0, 512),))
-        quantise(0, 2)
-        group_up(0, 16, CB)
-        quantise(0, 0, ((512, 1024), (1024, COLS)))
-
-        for ch in range(NCH):
-            nxt = ch + 1
-            more = nxt < NCH
-            if ch + 2 < NCH:
-                load_x2(ch + 2)
-                load_raw(ch + 2)
-            if more:
-                turn_in(nxt, 0, 2)
-                group_up(nxt, 0, 16)
-            multiply(ch, 0, (0, 1), () if more else (1,))
-            if more:
-                turn_in(nxt, 2, 4)
-                group_up(nxt, 16, CB)
-            multiply(ch, 0, (2, 3), () if more else (3,))
-            if ch == 0:
+        for u in range(NU):
+            if u % 2 == 1 and (u + 5) // 2 < NCH:
+                load_x2((u + 5) // 2)
+            if u + LEAD < NU:
+                load_raw(u + LEAD)
+            banks = []
+            if u == 0:
+                banks = banks_of(1)
+            elif (u + 3) // 2 < NCH:
+                banks = banks_of((u + 3) // 2)
+                half = len(banks) // 2
+                banks = (banks[0:half], banks[half:])[(u + 3) % 2]
+            bring = [(turn_in, bank + (k in V_SHARE.get(u, ()),)) for k, bank in enumerate(banks)]
+            if u + 2 < NU:
+                bring += [(pass_through, (u + 2, g, x0, x1)) for g in others_of(u + 2)[1:] for x0, x1 in X_CUTS]
+            groups = [(multiply, (u, lo, hi, j, u == NU - 1 and j % 2 == 1)) for lo, hi in CUTS[u % 2] for j in range(NJ)]
+            steps = []
+            if u == 0:
+                steps, groups = groups, []
+            while groups or bring:
+                steps += bring[0:2] + groups[0:2]
+                groups, bring = groups[2:], bring[2:]
+            for stage, args in steps:
+                stage(*args)
+            if u + 2 < NU:
+                regroup(u + 2)
+            if u + 1 < NU:
+                prepare(u + 1)
+            if u == 0:
                 make_gate()
-            if more:
-                turn_in(nxt, 4, 6)
-                quantise(nxt, 0)
-            finish(ch, 0, range(NJ))
-            if not more:
-                store(ch, 0, 14)
-            multiply(ch, 1, (0, 1), () if more else (1,))
-            if more:
-                turn_in(nxt, 6, 8)
-                quantise(nxt, 1)
-            multiply(ch, 1, (2, 3), () if more else (3,))
-            if more:
-                turn_in(nxt, 8, 10)
-            finish(ch, 1, range(NJ))
-            multiply(ch, 2, range(NJ), () if more else (1, 3))
-            store(ch, 0 if more else 14, 28)
-            if more:
-                quantise(nxt, 2)
-            finish(ch, 2, range(NJ))
-            store(ch, 28, CB)
+                late_wgs = [(k, turn_w(*k)) for k in late]
+                for k, wg in late_wgs:
+                    quantise_w(k, wg)
+            if u > 0:
+                s0, s1 = SAMPLES[(u - 1) % 2]
+                finish(u - 1, s0, s1, S_SAMPLES.get(u - 1, 0), False)
+                store(u - 1, s0, s1)
+        for s0, s1 in ((14, 20), (20, 26), (26, CB)):
+            finish(NU - 1, s0, s1, 0, True)
+            store(NU - 1, s0, s1)

@@ -28,10 +28,10 @@ CUTS = (((0, 512),), ((512, 1024), (1024, COLS)))
 SAMPLES = ((0, 14), (14, CB))
 Y_SHIFT = 8
 G_ORDER = (0, 1, 2)
-TURNED = ((1, 2), (1, 2), (1, 2), (1, 2))
+TURNED = ((2,), (1, 2), (2,), (2,))
 LEAD = 4
 V_SHARE = {0: (0, 2, 4, 6, 8)}
-S_SAMPLES = {5: 4, 6: 4}
+S_SAMPLES = {}
 
 FLOPS = 2 * C * C3 * B * PX + 2 * B * C * C
 
@@ -43,7 +43,7 @@ def tile_joint_module_pa_t_kernel(tc, fv, ft, W1, b1, g1, be1, m1, v1, Wfc1, bfc
         psum_t = ctx.enter_context(tc.psum_pool(name="psum_t", bufs=3))
         psum_m = ctx.enter_context(tc.psum_pool(name="psum_m", bufs=5))
         x2_pool = ctx.enter_context(tc.tile_pool(name="x2", bufs=4))
-        raw_pool = ctx.enter_context(tc.tile_pool(name="raw", bufs=5))
+        raw_pool = ctx.enter_context(tc.tile_pool(name="raw", bufs=7))
         grp_pool = ctx.enter_context(tc.tile_pool(name="grp", bufs=6))
         code_pool = ctx.enter_context(tc.tile_pool(name="code", bufs=2))
         ost_pool = ctx.enter_context(tc.tile_pool(name="ost", bufs=2))
@@ -91,12 +91,12 @@ def tile_joint_module_pa_t_kernel(tc, fv, ft, W1, b1, g1, be1, m1, v1, Wfc1, bfc
 
         w1_sb = ost_pool.tile([P, NJ * C3], BF16, tag="ost")
         nc.sync.dma_start(out=w1_sb[:], in_=W1.rearrange("(o j) c -> o (j c)", j=NJ))
-        for i, vec in enumerate((b1, g1, be1, m1, v1, bfc1)):
-            nc.scalar.dma_start(out=vec_rows[i : i + 1, :], in_=vec.rearrange("(o c) -> o c", o=1))
         ft_sb = keep.tile([P, C], BF16)
         wfc_sb = keep.tile([P, NJ, C], BF16)
         load_x2(0)
         load_raw(0)
+        for i, vec in enumerate((b1, g1, be1, m1, v1, bfc1)):
+            nc.sync.dma_start(out=vec_rows[i : i + 1, :], in_=vec.rearrange("(o c) -> o c", o=1))
         load_raw(1)
         load_x2(1)
         load_raw(2)
@@ -341,8 +341,11 @@ def tile_joint_module_pa_t_kernel(tc, fv, ft, W1, b1, g1, be1, m1, v1, Wfc1, bfc
                 )
 
         for i, bank in enumerate(banks_of(0)):
-            turn_in(*bank, i in (1, 3, 5, 7))
+            turn_in(*bank, i in (1, 3))
         regroup(0)
+        for g in others_of(0)[1:]:
+            for x0, x1 in X_CUTS:
+                pass_through(0, g, x0, x1)
         make_batch_norm()
         prepare(0)
         load_x2(2)
@@ -361,6 +364,8 @@ def tile_joint_module_pa_t_kernel(tc, fv, ft, W1, b1, g1, be1, m1, v1, Wfc1, bfc
                 half = len(banks) // 2
                 banks = (banks[0:half], banks[half:])[(u + 3) % 2]
             bring = [(turn_in, bank + (k in V_SHARE.get(u, ()),)) for k, bank in enumerate(banks)]
+            if u == 0:
+                bring = [(pass_through, (1, g, x0, x1)) for g in others_of(1)[1:] for x0, x1 in X_CUTS] + bring
             if u + 2 < NU:
                 bring += [(pass_through, (u + 2, g, x0, x1)) for g in others_of(u + 2)[1:] for x0, x1 in X_CUTS]
             groups = [(multiply, (u, lo, hi, j, u == NU - 1 and j % 2 == 1)) for lo, hi in CUTS[u % 2] for j in range(NJ)]

@@ -28,10 +28,10 @@ CUTS = (((0, 512),), ((512, 1024), (1024, COLS)))
 SAMPLES = ((0, 14), (14, CB))
 Y_SHIFT = 8
 G_ORDER = (0, 1, 2)
-TURNED = ((2,), (1, 2), (2,), (2,))
+TURNED = ((2,), (2,), (2,), (2,))
 LEAD = 4
-V_SHARE = {0: (0, 2, 4, 6, 8)}
-S_SAMPLES = {}
+V_SHARE = {}
+S_SAMPLES = {5: 3, 6: 4}
 
 FLOPS = 2 * C * C3 * B * PX + 2 * B * C * C
 
@@ -42,8 +42,8 @@ def tile_joint_module_pa_t_kernel(tc, fv, ft, W1, b1, g1, be1, m1, v1, Wfc1, bfc
         keep = ctx.enter_context(tc.tile_pool(name="keep", bufs=1))
         psum_t = ctx.enter_context(tc.psum_pool(name="psum_t", bufs=3))
         psum_m = ctx.enter_context(tc.psum_pool(name="psum_m", bufs=5))
-        x2_pool = ctx.enter_context(tc.tile_pool(name="x2", bufs=4))
-        raw_pool = ctx.enter_context(tc.tile_pool(name="raw", bufs=7))
+        x2_pool = ctx.enter_context(tc.tile_pool(name="x2", bufs=3))
+        raw_pool = ctx.enter_context(tc.tile_pool(name="raw", bufs=8))
         grp_pool = ctx.enter_context(tc.tile_pool(name="grp", bufs=6))
         code_pool = ctx.enter_context(tc.tile_pool(name="code", bufs=2))
         ost_pool = ctx.enter_context(tc.tile_pool(name="ost", bufs=2))
@@ -178,27 +178,18 @@ def tile_joint_module_pa_t_kernel(tc, fv, ft, W1, b1, g1, be1, m1, v1, Wfc1, bfc
         def others_of(u):
             return [g for g in range(NG) if g not in TURNED[u // 2]]
 
+        def regroup_part(u, g, b0, b1, on_vector):
+            copy(
+                on_vector,
+                unit_of(u, g)[:, b0:b1].rearrange("p b (q i) t -> p b q t i", i=4),
+                raws[(u, g)][:, b0:b1].rearrange("p b (t q i) -> p b q t i", t=4, i=4),
+            )
+
         def regroup(u):
             for g in others_of(u)[0:1]:
-                nc.vector.tensor_copy(
-                    out=unit_of(u, g).rearrange("p b (q i) t -> p b q t i", i=4),
-                    in_=raws[(u, g)][:].rearrange("p b (t q i) -> p b q t i", t=4, i=4),
-                )
-
-        X_CUTS = ((0, 16), (16, 32), (32, PX))
-
-        def pass_through(u, g, x0, x1):
-            src = raws[(u, g)][:].rearrange("p b (t x) -> p b x t", t=4)
-            n = 8 * (x1 - x0) * 4
-            pin = psum_t.tile([P, 2, 512], BF16, tag="bank")
-            for k in range(2):
-                nc.tensor.matmul(
-                    pin[:, k, 0:n], lhsT=ident_bf[:], rhs=src[:, 8 * k : 8 * k + 8, x0:x1], start=True, stop=True
-                )
-            nc.scalar.copy(
-                out=unit_of(u, g)[:, :, x0:x1].rearrange("p (k b) x t -> p k b (x t)", k=2),
-                in_=pin[:, :, 0:n].rearrange("p k (b n) -> p k b n", b=8),
-            )
+                regroup_part(u, g, 0, HB, True)
+            for g in others_of(u)[1:]:
+                regroup_part(u, g, 0, 8, True)
 
         def prepare(u):
             ch = u // 2
@@ -344,8 +335,7 @@ def tile_joint_module_pa_t_kernel(tc, fv, ft, W1, b1, g1, be1, m1, v1, Wfc1, bfc
             turn_in(*bank, i in (1, 3))
         regroup(0)
         for g in others_of(0)[1:]:
-            for x0, x1 in X_CUTS:
-                pass_through(0, g, x0, x1)
+            regroup_part(0, g, 8, HB, False)
         make_batch_norm()
         prepare(0)
         load_x2(2)
@@ -365,9 +355,9 @@ def tile_joint_module_pa_t_kernel(tc, fv, ft, W1, b1, g1, be1, m1, v1, Wfc1, bfc
                 banks = (banks[0:half], banks[half:])[(u + 3) % 2]
             bring = [(turn_in, bank + (k in V_SHARE.get(u, ()),)) for k, bank in enumerate(banks)]
             if u == 0:
-                bring = [(pass_through, (1, g, x0, x1)) for g in others_of(1)[1:] for x0, x1 in X_CUTS] + bring
+                bring = [(regroup_part, (1, g, 8, HB, False)) for g in others_of(1)[1:]] + bring
             if u + 2 < NU:
-                bring += [(pass_through, (u + 2, g, x0, x1)) for g in others_of(u + 2)[1:] for x0, x1 in X_CUTS]
+                bring += [(regroup_part, (u + 2, g, 8, HB, False)) for g in others_of(u + 2)[1:]]
             groups = [(multiply, (u, lo, hi, j, u == NU - 1 and j % 2 == 1)) for lo, hi in CUTS[u % 2] for j in range(NJ)]
             steps = []
             if u == 0:

from contextlib import ExitStack

import concourse.mybir as mybir
from concourse.masks import make_identity

F32 = mybir.dt.float32
BF16 = mybir.dt.bfloat16
U32 = mybir.dt.uint32
U8 = mybir.dt.uint8
FP8X4 = mybir.dt.float8_e4m3fn_x4
ALU = mybir.AluOpType
ACT = mybir.ActivationFunctionType

P = 128
B, C, PX = 128, 512, 36
C3 = 3 * C
EPS = 1e-5
NG = 3
NJ = 4
CB = 32
NCH = B // CB
LAST = NCH - 1
HB = CB // 2
NU = B // HB
NR = PX // 2
COLS = CB * PX
CUTS = (((0, 512),), ((512, 1024), (1024, COLS)))
SAMPLES = ((0, 14), (14, CB))
Y_SHIFT = 8
G_ORDER = (0, 1, 2)
TURNED = ((2,), (2,), (2,), (2,))
LEAD = 4
V_SHARE = {}
S_SAMPLES = {5: 3, 6: 4}

FLOPS = 2 * C * C3 * B * PX + 2 * B * C * C


def tile_joint_module_pa_t_kernel(tc, fv, ft, W1, b1, g1, be1, m1, v1, Wfc1, bfc1, out):
    nc = tc.nc
    with ExitStack() as ctx:
        keep = ctx.enter_context(tc.tile_pool(name="keep", bufs=1))
        psum_t = ctx.enter_context(tc.psum_pool(name="psum_t", bufs=3))
        psum_m = ctx.enter_context(tc.psum_pool(name="psum_m", bufs=5))
        x2_pool = ctx.enter_context(tc.tile_pool(name="x2", bufs=3))
        raw_pool = ctx.enter_context(tc.tile_pool(name="raw", bufs=8))
        grp_pool = ctx.enter_context(tc.tile_pool(name="grp", bufs=6))
        code_pool = ctx.enter_context(tc.tile_pool(name="code", bufs=2))
        ost_pool = ctx.enter_context(tc.tile_pool(name="ost", bufs=2))
        ctx.enter_context(tc.manual_schedule())

        ident_bf = keep.tile([P, P], BF16)
        make_identity(nc, ident_bf[:])
        ident_f = keep.tile([P, P], F32)
        make_identity(nc, ident_f[:])
        gate = keep.tile([P, NJ, B], F32)
        bn_scale = keep.tile([P, NJ], F32)
        bn_shift = keep.tile([P, NJ], F32)
        y = keep.tile([P, NJ, COLS + Y_SHIFT * LAST], F32)
        warm = keep.tile([P, 1], F32)
        nc.vector.memset(warm[:], 1.0)
        nc.scalar.sqrt(warm[:], warm[:])
        vec_rows = keep.tile([P, C], BF16)
        nc.vector.memset(vec_rows[:], 0.0)

        x2s, raws, grps, codes_of, osts = {}, {}, {}, {}, {}

        def load_turned(ch, g):
            x2c = x2_pool.tile([P, P * PX], BF16, tag="x2c")
            for t in range(4):
                c0 = g * C + t * P
                nc.sync.dma_start(
                    out=x2c[t : P : 4, :],
                    in_=fv[ch * CB : (ch + 1) * CB, c0 : c0 + P].rearrange("b c h w -> b (c h w)"),
                )
            x2s[(ch, g)] = x2c

        def load_x2(ch):
            for g in TURNED[ch]:
                load_turned(ch, g)

        def load_raw(u):
            for g in range(NG):
                if g not in TURNED[u // 2]:
                    raw = raw_pool.tile([P, HB, 4 * PX], BF16, tag="raw")
                    nc.sync.dma_start(
                        out=raw[:],
                        in_=fv[u * HB : (u + 1) * HB, g * C : (g + 1) * C].rearrange("b (p t) h w -> p b (t h w)", t=4),
                    )
                    raws[(u, g)] = raw

        w1_sb = ost_pool.tile([P, NJ * C3], BF16, tag="ost")
        nc.sync.dma_start(out=w1_sb[:], in_=W1.rearrange("(o j) c -> o (j c)", j=NJ))
        ft_sb = keep.tile([P, C], BF16)
        wfc_sb = keep.tile([P, NJ, C], BF16)
        load_x2(0)
        load_raw(0)
        for i, vec in enumerate((b1, g1, be1, m1, v1, bfc1)):
            nc.sync.dma_start(out=vec_rows[i : i + 1, :], in_=vec.rearrange("(o c) -> o c", o=1))
        load_raw(1)
        load_x2(1)
        load_raw(2)
        nc.sync.dma_start(out=ft_sb[:], in_=ft)
        nc.sync.dma_start(out=wfc_sb[:], in_=Wfc1.rearrange("(o j) k -> o j k", j=NJ))
        load_raw(3)

        w_words = w1_sb[:].bitcast(F32).rearrange("o (j g p u) -> o j g u p", j=NJ, g=NG, p=P, u=2)
        w_of = {}

        def copy(on_vector, dst, src):
            if on_vector:
                nc.vector.tensor_copy(out=dst, in_=src)
            else:
                nc.scalar.copy(out=dst, in_=src)

        def turn_w(g, turned):
            wg = grp_pool.tile([P, 4 * C], BF16, tag="grp", align_bytes=64)
            if turned:
                for j in range(NJ):
                    pk = psum_m.tile([P, 4, P], BF16, tag="bank")
                    for t in range(4):
                        c0 = j * C3 + g * C + t * P
                        nc.tensor.transpose(pk[:, t, :], w1_sb[:, c0 : c0 + P], ident_bf[:])
                    dst = wg[:].rearrange("p (j o t) -> p j o t", j=NJ, o=P, t=4)[:, j]
                    copy(j % 2 == 0, dst, pk[:].rearrange("p t o -> p o t"))
            else:
                for jp in range(NJ // 2):
                    pw = psum_m.tile([P, 2, 2, P], F32, tag="bank")
                    for jj in range(2):
                        for w in range(2):
                            nc.tensor.transpose(pw[:, jj, w, :], w_words[:, 2 * jp + jj, g, w, :], ident_f[:])
                    dst = wg[:].bitcast(F32).rearrange("p (j o w) -> p j o w", j=NJ, o=P, w=2)
                    copy(jp == 0, dst[:, 2 * jp : 2 * jp + 2], pw[:].rearrange("p j w o -> p j o w"))
            return wg

        def quantise_w(key, wg):
            codes = keep.tile([P, C], U32, align_bytes=64, name="w_codes_%d_%d" % (key[0], int(key[1])))
            scales = keep.tile([P, C], U8, align_bytes=64, name="w_scales_%d_%d" % (key[0], int(key[1])))
            nc.vector.quantize_mx(out=codes[:].bitcast(FP8X4), scales=scales[:], in_=wg[:])
            w_of[key] = (codes, scales)

        need = [(g, turned) for turned in (True, False) for g in range(NG) if any((g in TURNED[ch]) == turned for ch in range(NCH))]
        early = [k for k in need if (k[0] in TURNED[0]) == k[1]]
        late = [k for k in need if k not in early]
        wgs = [(k, turn_w(*k)) for k in early]
        for k, wg in wgs:
            quantise_w(k, wg)

        def group_tile(ch, g):
            if (ch, g) not in grps:
                grp = grp_pool.tile([P, 4 * COLS], BF16, tag="grp", align_bytes=64)
                grps[(ch, g)] = grp
            return grps[(ch, g)]

        def banks_of(ch):
            return [(ch, g, r0) for g in TURNED[ch] for r0 in range(0, NR, 4)]

        def turn_in(ch, g, r0, on_vector):
            nr = min(4, NR - r0)
            words = x2s[(ch, g)][:].bitcast(F32).rearrange("p (c r) -> p r c", r=NR)
            pin = psum_t.tile([P, 4, P], F32, tag="bank")
            for k in range(nr):
                nc.tensor.transpose(pin[:, k, :], words[:, r0 + k, :], ident_f[:])
            dst = group_tile(ch, g)[:].rearrange("p (b r e t) -> p r b e t", b=CB, r=NR, e=2, t=4)[:, r0 : r0 + nr]
            src = (
                pin[:, 0:nr, :]
                .rearrange("p r w -> p (r w)")
                .bitcast(BF16)
                .rearrange("p (r b t e) -> p r b e t", r=nr, b=CB, t=4)
            )
            copy(on_vector, dst, src)

        def unit_of(u, g):
            return group_tile(u // 2, g)[:].rearrange("p (b x t) -> p b x t", b=CB, t=4)[
                :, (u % 2) * HB : (u % 2 + 1) * HB
            ]

        def others_of(u):
            return [g for g in range(NG) if g not in TURNED[u // 2]]

        def regroup_part(u, g, b0, b1, on_vector):
            copy(
                on_vector,
                unit_of(u, g)[:, b0:b1].rearrange("p b (q i) t -> p b q t i", i=4),
                raws[(u, g)][:, b0:b1].rearrange("p b (t q i) -> p b q t i", t=4, i=4),
            )

        def regroup(u):
            for g in others_of(u)[0:1]:
                regroup_part(u, g, 0, HB, True)
            for g in others_of(u)[1:]:
                regroup_part(u, g, 0, 8, True)

        def prepare(u):
            ch = u // 2
            if ch not in codes_of:
                codes = code_pool.tile([P, NG, COLS], U32, align_bytes=64)
                scales = code_pool.tile([P, NG, COLS], U8, align_bytes=64)
                codes_of[ch] = (codes, scales)
            codes, scales = codes_of[ch]
            for g in G_ORDER:
                for lo, hi in CUTS[u % 2]:
                    nc.vector.quantize_mx(
                        out=codes[:, g, lo:hi].bitcast(FP8X4),
                        scales=scales[:, g, lo:hi],
                        in_=grps[(ch, g)][:, 4 * lo : 4 * hi],
                    )

        def multiply(u, lo, hi, j, on_vector):
            ch = u // 2
            codes, scales = codes_of[ch]
            acc = psum_m.tile([P, 512], F32, tag="bank")
            for g in G_ORDER:
                wc, ws = w_of[(g, g in TURNED[ch])]
                nc.tensor.matmul_mx(
                    out=acc[:, 0 : hi - lo],
                    lhsT=wc[:, j * P : (j + 1) * P].bitcast(FP8X4),
                    lhsT_scale=ws[:, j * P : (j + 1) * P],
                    rhs=codes[:, g, lo:hi].bitcast(FP8X4),
                    rhs_scale=scales[:, g, lo:hi],
                    start=(g == G_ORDER[0]),
                    stop=(g == G_ORDER[-1]),
                )
            y0 = Y_SHIFT * (LAST - ch)
            dst = y[:, j, y0 + lo : y0 + hi]
            if on_vector:
                nc.vector.tensor_scalar(
                    out=dst,
                    in0=acc[:, 0 : hi - lo],
                    scalar1=bn_scale[:, j : j + 1],
                    scalar2=bn_shift[:, j : j + 1],
                    op0=ALU.mult,
                    op1=ALU.add,
                )
            else:
                nc.scalar.activation(
                    out=dst,
                    in_=acc[:, 0 : hi - lo],
                    func=ACT.Relu,
                    bias=bn_shift[:, j : j + 1],
                    scale=bn_scale[:, j : j + 1],
                )

        def finish(u, s0, s1, on_scalar, with_relu):
            ch = u // 2
            if ch not in osts:
                ost = ost_pool.tile([P, CB, NJ, PX], F32, tag="ost")
                osts[ch] = ost
            ost = osts[ch]
            y0 = Y_SHIFT * (LAST - ch)
            for b in range(s1 - on_scalar, s1):
                for j in range(NJ):
                    nc.scalar.activation(
                        out=ost[:, b, j, :],
                        in_=y[:, j, y0 + b * PX : y0 + (b + 1) * PX],
                        func=ACT.Copy,
                        scale=gate[:, j, ch * CB + b : ch * CB + b + 1],
                    )
            s1 -= on_scalar
            yv = y[:, :, y0 + s0 * PX : y0 + s1 * PX].rearrange("p j (b x) -> p j b x", x=PX)
            gv = gate[:, :, ch * CB + s0 : ch * CB + s1].unsqueeze(3)
            if with_relu:
                for j in range(NJ):
                    nc.vector.scalar_tensor_tensor(
                        out=ost[:, s0:s1, j, :],
                        in0=yv[:, j],
                        scalar=0.0,
                        in1=gv[:, j].to_broadcast([P, s1 - s0, PX]),
                        op0=ALU.max,
                        op1=ALU.mult,
                    )
            else:
                nc.vector.tensor_tensor(
                    out=ost[:, s0:s1].rearrange("p b j x -> p j b x"),
                    in0=yv,
                    in1=gv.to_broadcast([P, NJ, s1 - s0, PX]),
                    op=ALU.mult,
                )

        def store(u, s0, s1):
            b0 = (u // 2) * CB
            nc.sync.dma_start(
                out=out[b0 + s0 : b0 + s1].rearrange("b (p j) h w -> p b (j h w)", j=NJ),
                in_=osts[u // 2][:, s0:s1].rearrange("p b j x -> p b (j x)"),
            )

        vecs = keep.tile([P, 6, NJ], F32)
        std = keep.tile([P, NJ], F32)
        rstd = keep.tile([P, NJ], F32)
        diff = keep.tile([P, NJ], F32)

        def make_batch_norm():
            pv = psum_t.tile([P, NJ, P], BF16, tag="bank")
            for j in range(NJ):
                nc.tensor.transpose(pv[:, j, :], vec_rows[:, j : C : NJ], ident_bf[:])
            nc.vector.tensor_copy(out=vecs[:].rearrange("p i j -> p j i"), in_=pv[:, :, 0:6])
            nc.vector.tensor_scalar_add(out=std[:], in0=vecs[:, 4], scalar1=EPS)
            nc.scalar.sqrt(std[:], std[:])
            nc.vector.reciprocal(rstd[:], std[:])
            nc.vector.tensor_mul(out=bn_scale[:], in0=vecs[:, 1], in1=rstd[:])
            nc.vector.tensor_sub(out=diff[:], in0=vecs[:, 0], in1=vecs[:, 3])
            nc.vector.tensor_mul(out=diff[:], in0=diff[:], in1=bn_scale[:])
            nc.vector.tensor_add(out=bn_shift[:], in0=diff[:], in1=vecs[:, 2])

        ftT = keep.tile([P, NJ, P], BF16)
        wfcT = keep.tile([P, NJ, NJ, P], BF16)

        def make_gate():
            pt = psum_t.tile([P, NJ, P], BF16, tag="bank")
            for kc in range(NJ):
                nc.tensor.transpose(pt[:, kc, :], ft_sb[:, kc * P : (kc + 1) * P], ident_bf[:])
            nc.scalar.copy(out=ftT[:], in_=pt[:])
            for kc in range(NJ):
                pk = psum_t.tile([P, NJ, P], BF16, tag="bank")
                for j in range(NJ):
                    nc.tensor.transpose(pk[:, j, :], wfc_sb[:, j, kc * P : (kc + 1) * P], ident_bf[:])
                nc.scalar.copy(out=wfcT[:, kc], in_=pk[:])
            pf = psum_t.tile([P, NJ, P], F32, tag="bank")
            for j in range(NJ):
                for kc in range(NJ):
                    nc.tensor.matmul(
                        pf[:, j, :], lhsT=wfcT[:, kc, j, :], rhs=ftT[:, kc, :], start=(kc == 0), stop=(kc == NJ - 1)
                    )
            for j in range(NJ):
                nc.vector.tensor_scalar(
                    out=gate[:, j, :],
                    in0=pf[:, j, :],
                    scalar1=vecs[:, 5, j : j + 1],
                    scalar2=1.0,
                    op0=ALU.add,
                    op1=ALU.add,
                )

        for i, bank in enumerate(banks_of(0)):
            turn_in(*bank, i in (1, 3))
        regroup(0)
        for g in others_of(0)[1:]:
            regroup_part(0, g, 8, HB, False)
        make_batch_norm()
        prepare(0)
        load_x2(2)
        regroup(1)

        for u in range(NU):
            if u % 2 == 1 and (u + 5) // 2 < NCH:
                load_x2((u + 5) // 2)
            if u + LEAD < NU:
                load_raw(u + LEAD)
            banks = []
            if u == 0:
                banks = banks_of(1)
            elif (u + 3) // 2 < NCH:
                banks = banks_of((u + 3) // 2)
                half = len(banks) // 2
                banks = (banks[0:half], banks[half:])[(u + 3) % 2]
            bring = [(turn_in, bank + (k in V_SHARE.get(u, ()),)) for k, bank in enumerate(banks)]
            if u == 0:
                bring = [(regroup_part, (1, g, 8, HB, False)) for g in others_of(1)[1:]] + bring
            if u + 2 < NU:
                bring += [(regroup_part, (u + 2, g, 8, HB, False)) for g in others_of(u + 2)[1:]]
            groups = [(multiply, (u, lo, hi, j, u == NU - 1 and j % 2 == 1)) for lo, hi in CUTS[u % 2] for j in range(NJ)]
            steps = []
            if u == 0:
                steps, groups = groups, []
            while groups or bring:
                steps += bring[0:2] + groups[0:2]
                groups, bring = groups[2:], bring[2:]
            for stage, args in steps:
                stage(*args)
            if u + 2 < NU:
                regroup(u + 2)
            if u + 1 < NU:
                prepare(u + 1)
            if u == 0:
                make_gate()
                late_wgs = [(k, turn_w(*k)) for k in late]
                for k, wg in late_wgs:
                    quantise_w(k, wg)
            if u > 0:
                s0, s1 = SAMPLES[(u - 1) % 2]
                finish(u - 1, s0, s1, S_SAMPLES.get(u - 1, 0), False)
                store(u - 1, s0, s1)
        for s0, s1 in ((14, 20), (20, 26), (26, CB)):
            finish(NU - 1, s0, s1, 0, True)
            store(NU - 1, s0, s1)
